import numpy as np
import ml_dtypes


def mxq(x, axis, fmt="e4m3"):
    dtype, down = {"e4m3": (ml_dtypes.float8_e4m3fn, 7), "e5m2": (ml_dtypes.float8_e5m2, 14)}[fmt]
    v = np.moveaxis(np.asarray(x, np.float32).astype(ml_dtypes.bfloat16).astype(np.float64), axis, -1)
    blocks = v.reshape(v.shape[:-1] + (-1, 32))
    amax = np.abs(blocks).max(-1, keepdims=True)
    byte = np.maximum(np.where(amax > 0, np.frexp(amax)[1] - 1 + 127, 0) - down, 1)
    scale = np.exp2(byte - 127.0)
    codes = (blocks / scale).astype(np.float32).astype(dtype).astype(np.float64)
    return np.moveaxis((codes * scale).reshape(v.shape), -1, axis)


WIDE = False


def mx_kscale(k):
    if not WIDE:
        return np.ones(k)
    levels = np.array([10, -10, 5, -5, 0])
    a = np.random.permutation(np.resize(levels, k // 512 * 4)).reshape(k // 512, 4)
    idx = np.arange(k)
    return np.exp2(a[idx // 512, idx % 128 // 32])


BF16 = ml_dtypes.bfloat16


def bf(x):
    return np.asarray(x, np.float32).astype(BF16)


def f64(x):
    return np.asarray(x).astype(np.float64)


E2M1 = np.array([0.0, 0.5, 1.0, 1.5, 2.0, 3.0, 4.0, 6.0, -0.0, -0.5, -1.0, -1.5, -2.0, -3.0, -4.0, -6.0])


def pack_weight(w, fmt):
    k, n = w.shape
    w = f64(bf(w)).reshape(k // 32, 32, n)
    amax = np.abs(w).max(1)
    if fmt == "e4m3":
        byte = np.frexp(amax)[1] - 1 + 127 - 7
    else:
        mant, ex = np.frexp(amax / 6.0)
        byte = np.where(mant > 0.5, ex, ex - 1) + 127
    byte = np.clip(np.where(amax > 0, byte, 1), 1, 254)
    scaled = (w * np.exp2(127.0 - byte)[:, None, :]).reshape(k, n).astype(np.float32)
    by_word = np.ascontiguousarray(scaled.reshape(k // 512, 128, 4, n).transpose(0, 1, 3, 2))
    if fmt == "e4m3":
        words = by_word.astype(ml_dtypes.float8_e4m3fn).view(np.uint8)
    else:
        c = by_word.astype(ml_dtypes.float4_e2m1fn).view(np.uint8) & 0xF
        words = c[..., 0::2] | (c[..., 1::2] << 4)
    return np.ascontiguousarray(words), np.ascontiguousarray(byte.astype(np.uint8).reshape(k // 512, 16, n))


def unpack_weight(words, scales, fmt):
    g, p, n, _ = words.shape
    if fmt == "e4m3":
        vals = np.ascontiguousarray(words).view(ml_dtypes.float8_e4m3fn).astype(np.float64)
    else:
        nib = np.empty((g, p, n, 4), np.uint8)
        nib[..., 0::2] = words & 0xF
        nib[..., 1::2] = words >> 4
        vals = E2M1[nib]
    vals = vals * np.repeat(np.exp2(scales.astype(np.float64) - 127.0), 8, axis=1)[..., None]
    return vals.transpose(0, 1, 3, 2).reshape(g * 512, n)


B, D, O1, O2, O3 = 4096, 1024, 1024, 256, 128
EPS = 1e-5
FMT = "e4m3"


def mish(v):
    return v * np.tanh(np.log(1.0 + np.exp(v)))


def ln(u, g, b):
    mu = u.mean(-1, keepdims=True)
    var = np.square(u - mu).mean(-1, keepdims=True)
    return (u - mu) * (1.0 / np.sqrt(var + EPS)) * g + b


def setup_inputs():
    s = mx_kscale(D)
    x = bf(np.random.uniform(0.0, 1.0, (B, D)) * s)
    w1 = np.random.standard_normal((O1, D)) * 1.5 / np.sqrt(D) / s
    W1_words, W1_scales = pack_weight(np.ascontiguousarray(w1.T), FMT)
    g1 = bf(1.0 + 0.1 * np.random.standard_normal(O1))
    b1 = bf(0.1 * np.random.standard_normal(O1))
    w2 = np.random.standard_normal((O2, O1)) * 1.5 / np.sqrt(O1)
    W2_words, W2_scales = pack_weight(np.ascontiguousarray(w2.T), FMT)
    g2 = bf(1.0 + 0.1 * np.random.standard_normal(O2))
    b2 = bf(0.1 * np.random.standard_normal(O2))
    return {"x": x,
            "W1_words": W1_words,
            "W1_scales": W1_scales,
            "g1": g1,
            "b1": b1,
            "W2_words": W2_words,
            "W2_scales": W2_scales,
            "g2": g2,
            "b2": b2}


def reference(x, W1_words, W1_scales, g1, b1, W2_words, W2_scales, g2, b2):
    u1 = mxq(f64(x), 1, "e4m3") @ unpack_weight(W1_words, W1_scales, FMT)
    h1 = mish(ln(u1, f64(g1), f64(b1)))
    u2 = mxq(h1, 1, "e4m3") @ unpack_weight(W2_words, W2_scales, FMT)
    return mish(ln(u2, f64(g2), f64(b2)))

@@ -1,0 +1,373 @@
+from contextlib import ExitStack
+
+import concourse.mybir as mybir
+from concourse.masks import make_identity
+
+F32 = mybir.dt.float32
+BF16 = mybir.dt.bfloat16
+I32 = mybir.dt.int32
+U32 = mybir.dt.uint32
+U8 = mybir.dt.uint8
+FP8X4 = mybir.dt.float8_e4m3fn_x4
+ACT = mybir.ActivationFunctionType
+ALU = mybir.AluOpType
+
+P = 128
+PACK = 4
+K_PASS = P * PACK
+TOKENS, D_IN, D_HID, D_OUT = 4096, 1024, 1024, 256
+WORDS = K_PASS // 2
+PASSES = D_IN // K_PASS
+HALVES = D_HID // K_PASS
+N_TILES = TOKENS // P
+BATCH = 4
+N_BATCH = N_TILES // BATCH
+EPS = 1e-5
+STATS = 6
+
+FLOPS = 2 * TOKENS * D_IN * D_HID + 2 * TOKENS * D_HID * D_OUT
+
+
+def tile_autoencoder_pa_t_kernel(
+    tc, x, W1_words, W1_scales, g1, b1, W2_words, W2_scales, g2, b2, out
+):
+    nc = tc.nc
+    with ExitStack() as stack:
+        const = stack.enter_context(tc.tile_pool(name="const", bufs=1))
+        pair = stack.enter_context(tc.tile_pool(name="pair", bufs=2))
+        triple = stack.enter_context(tc.tile_pool(name="triple", bufs=3))
+        quad = stack.enter_context(tc.tile_pool(name="quad", bufs=BATCH))
+        small = stack.enter_context(tc.tile_pool(name="small", bufs=4))
+        psum_u1 = stack.enter_context(tc.psum_pool(name="psum_u1", bufs=2 * HALVES))
+        psum_ht = stack.enter_context(tc.psum_pool(name="psum_ht", bufs=2))
+        psum_xt = stack.enter_context(tc.psum_pool(name="psum_xt", bufs=1))
+        psum_u2 = stack.enter_context(tc.psum_pool(name="psum_u2", bufs=1))
+        stack.enter_context(tc.manual_schedule())
+
+        w1_scales = const.tile([P, PASSES, D_HID], U8, align_bytes=64)
+        w2_scales = const.tile([P, PASSES, D_OUT], U8, align_bytes=64)
+        nc.vector.memset(w1_scales[:].bitcast(I32), 0)
+        nc.vector.memset(w2_scales[:].bitcast(I32), 0)
+        w1_codes = const.tile([P, PASSES, PACK * D_HID], U8, align_bytes=64)
+        w2_codes = const.tile([P, PASSES, PACK * D_OUT], U8, align_bytes=64)
+
+        def load_scales(plane, scales):
+            for quadrant in range(4):
+                nc.sync.dma_start(
+                    out=plane[32 * quadrant : 32 * quadrant + 4, :, :].bitcast(I32),
+                    in_=scales[:, 4 * quadrant : 4 * quadrant + 4, :]
+                    .rearrange("g q n -> q g n")
+                    .bitcast(I32),
+                )
+
+        def load_codes(codes, words):
+            for g in range(PASSES):
+                nc.sync.dma_start(
+                    out=codes[:, g, :].bitcast(I32),
+                    in_=words[g].rearrange("p n t -> p (n t)").bitcast(I32),
+                )
+
+        x_rows = {}
+
+        def load_x(b):
+            if b >= N_BATCH:
+                return
+            x_rows[b] = pair.tile([P, BATCH, D_IN], BF16, name="x_rows")
+            for i in range(BATCH):
+                first = (b * BATCH + i) * P
+                nc.sync.dma_start(out=x_rows[b][:, i, :], in_=x[first : first + P, :])
+
+        load_scales(w1_scales, W1_scales)
+        load_x(0)
+        load_codes(w1_codes, W1_words)
+        load_scales(w2_scales, W2_scales)
+        load_codes(w2_codes, W2_words)
+
+        ident_f32 = const.tile([P, P], F32)
+        make_identity(nc, ident_f32[:])
+        ident_bf16 = const.tile([P, P], BF16)
+        make_identity(nc, ident_bf16[:])
+        half = const.tile([P, 1], F32)
+        nc.vector.memset(half[:], 0.5)
+        minus_half = const.tile([P, 1], F32)
+        nc.vector.memset(minus_half[:], -0.5)
+
+        raw_g1 = const.tile([P, D_HID], BF16)
+        raw_b1 = const.tile([P, D_HID], BF16)
+        raw_g2 = const.tile([P, D_OUT], BF16)
+        raw_b2 = const.tile([P, D_OUT], BF16)
+        for raw, vector in ((raw_g1, g1), (raw_b1, b1), (raw_g2, g2), (raw_b2, b2)):
+            nc.scalar.dma_start(out=raw[:], in_=vector.partition_broadcast(P))
+        gain1 = const.tile([P, HALVES, PACK, P], F32)
+        bias1 = const.tile([P, HALVES, PACK, P], F32)
+        gain2 = const.tile([P, D_OUT], F32)
+        bias2 = const.tile([P, D_OUT], F32)
+        for spread, raw in (
+            (gain1[:], raw_g1[:].rearrange("p (h m t) -> p h t m", h=HALVES, t=PACK)),
+            (bias1[:], raw_b1[:].rearrange("p (h m t) -> p h t m", h=HALVES, t=PACK)),
+            (gain2[:], raw_g2[:]),
+            (bias2[:], raw_b2[:]),
+        ):
+            nc.gpsimd.tensor_scalar(
+                out=spread, in0=raw, scalar1=1.0, scalar2=0.0, op0=ALU.mult, op1=ALU.add
+            )
+
+        def no_tile(n):
+            return n < 0 or n >= N_TILES
+
+        def no_batch(b):
+            return b < 0 or b >= N_BATCH
+
+        x_t, x_grouped, x_codes, x_scales = {}, {}, {}, {}
+        u1, rstd1, v1, e1 = {}, {}, {}, {}
+        h1, h1_t, h1_grouped, h1_codes, h1_scales = {}, {}, {}, {}, {}
+        u2, rstd2, v2, e2 = {}, {}, {}, {}
+
+        def transpose_x(n):
+            if no_tile(n):
+                return
+            words = x_rows[n // BATCH][:, n % BATCH, :].bitcast(F32)
+            x_t[n] = psum_xt.tile([P, PASSES, 2, P], F32, name="x_t")
+            for g in range(PASSES):
+                for u in range(2):
+                    nc.tensor.transpose(
+                        x_t[n][:, g, u, :],
+                        words[:, g * WORDS + u : (g + 1) * WORDS : 2],
+                        ident_f32[:],
+                    )
+
+        def regroup_x(n):
+            if no_tile(n):
+                return
+            x_grouped[n] = quad.tile([P, PASSES, P, PACK], BF16, name="x_grouped", align_bytes=64)
+            nc.scalar.copy(
+                out=x_grouped[n][:].bitcast(F32), in_=x_t[n][:].rearrange("p g u k -> p g k u")
+            )
+
+        def quantise(grouped, codes, scales):
+            nc.vector.quantize_mx(
+                out=codes.rearrange("p g k -> p (g k)").bitcast(FP8X4),
+                scales=scales.rearrange("p g k -> p (g k)"),
+                in_=grouped.rearrange("p g k t -> p (g k t)"),
+            )
+
+        def quantise_x(n):
+            if no_tile(n):
+                return
+            b, i = n // BATCH, n % BATCH
+            if i == 0:
+                x_codes[b] = pair.tile([P, BATCH, PASSES, P], U32, name="x_codes", align_bytes=64)
+                x_scales[b] = pair.tile([P, BATCH, PASSES, P], U8, name="x_scales", align_bytes=64)
+            quantise(x_grouped[n][:], x_codes[b][:, i], x_scales[b][:, i])
+
+        def layer1(n):
+            if no_tile(n):
+                return
+            b, i = n // BATCH, n % BATCH
+            for h in range(HALVES):
+                u1[n, h] = psum_u1.tile([P, K_PASS], F32, name="u1")
+                for g in range(PASSES):
+                    nc.tensor.matmul_mx(
+                        out=u1[n, h][:],
+                        lhsT=x_codes[b][:, i, g, :].bitcast(FP8X4),
+                        lhsT_scale=x_scales[b][:, i, g, :],
+                        rhs=w1_codes[:, g, PACK * K_PASS * h : PACK * K_PASS * (h + 1)].bitcast(FP8X4),
+                        rhs_scale=w1_scales[:, g, K_PASS * h : K_PASS * (h + 1)],
+                        start=(g == 0),
+                        stop=(g == PASSES - 1),
+                    )
+
+        def mean_and_inverse_std(banks):
+            stats = small.tile([P, len(banks), STATS], F32, name="stats")
+            for j, bank in enumerate(banks):
+                nc.vector.bn_stats(out=stats[:, j, :], in_=bank[:])
+            mean_var = small.tile([P, 2], F32, name="mean_var")
+            nc.vector.bn_aggr(out=mean_var[:], in_=stats[:].rearrange("p j s -> p (j s)"))
+            shifted = small.tile([P, 1], F32, name="shifted")
+            nc.gpsimd.tensor_scalar(
+                out=shifted[:], in0=mean_var[:, 1:2], scalar1=EPS, scalar2=1.0, op0=ALU.add, op1=ALU.mult
+            )
+            rstd = small.tile([P, 1], F32, name="rstd")
+            nc.gpsimd.tensor_tensor(out=rstd[:], in0=shifted[:], in1=minus_half[:], op=ALU.pow)
+            return mean_var[:, 0:1], rstd[:, 0:1]
+
+        def centre1(n):
+            if no_tile(n):
+                return
+            b, i = n // BATCH, n % BATCH
+            if i == 0:
+                v1[b] = triple.tile([P, BATCH, HALVES, PACK, P], F32, name="v1")
+            mean, rstd1[n] = mean_and_inverse_std([u1[n, h] for h in range(HALVES)])
+            for h in range(HALVES):
+                nc.vector.scalar_tensor_tensor(
+                    out=v1[b][:, i, h],
+                    in0=u1[n, h][:].rearrange("p (m t) -> p t m", t=PACK),
+                    scalar=mean,
+                    in1=gain1[:, h],
+                    op0=ALU.subtract,
+                    op1=ALU.mult,
+                )
+
+        def scale1(n):
+            if no_tile(n):
+                return
+            rows = v1[n // BATCH][:, n % BATCH].rearrange("p h t m -> p (h t m)")
+            nc.vector.scalar_tensor_tensor(
+                out=rows,
+                in0=rows,
+                scalar=rstd1[n],
+                in1=bias1[:].rearrange("p h t m -> p (h t m)"),
+                op0=ALU.mult,
+                op1=ALU.add,
+            )
+
+        def tanh_half(e, v):
+            nc.scalar.activation(out=e, in_=v, func=ACT.Tanh, scale=0.5)
+
+        def log_of_rest(e):
+            nc.scalar.activation(out=e, in_=e, func=ACT.Ln, scale=-0.5, bias=half[:, 0:1])
+
+        def tanh_softplus(e):
+            nc.scalar.activation(out=e, in_=e, func=ACT.Tanh, scale=-1.0)
+
+        def tanh_half1(n):
+            if no_tile(n):
+                return
+            b, i = n // BATCH, n % BATCH
+            if i == 0:
+                e1[b] = pair.tile([P, BATCH, D_HID], F32, name="e1")
+            tanh_half(e1[b][:, i, :], v1[b][:, i].rearrange("p h t m -> p (h t m)"))
+
+        def log_of_rest1(n):
+            if no_tile(n):
+                return
+            log_of_rest(e1[n // BATCH][:, n % BATCH, :])
+
+        def tanh_softplus1(n):
+            if no_tile(n):
+                return
+            tanh_softplus(e1[n // BATCH][:, n % BATCH, :])
+
+        def mish1(n):
+            if no_tile(n):
+                return
+            b, i = n // BATCH, n % BATCH
+            h1[n] = quad.tile([P, D_HID], BF16, name="h1")
+            nc.vector.tensor_tensor(
+                out=h1[n][:],
+                in0=v1[b][:, i].rearrange("p h t m -> p (h t m)"),
+                in1=e1[b][:, i, :],
+                op=ALU.mult,
+            )
+
+        def transpose_h1(n):
+            if no_tile(n):
+                return
+            h1_t[n] = psum_ht.tile([P, PASSES * PACK, P], BF16, name="h1_t")
+            for c in range(PASSES * PACK):
+                nc.tensor.transpose(h1_t[n][:, c, :], h1[n][:, c * P : (c + 1) * P], ident_bf16[:])
+
+        def regroup_h1(n):
+            if no_tile(n):
+                return
+            h1_grouped[n] = quad.tile([P, PASSES, P, PACK], BF16, name="h1_grouped", align_bytes=64)
+            nc.scalar.copy(
+                out=h1_grouped[n][:], in_=h1_t[n][:].rearrange("p (g t) k -> p g k t", t=PACK)
+            )
+
+        def quantise_h1(n):
+            if no_tile(n):
+                return
+            h1_codes[n] = pair.tile([P, PASSES, P], U32, name="h1_codes", align_bytes=64)
+            h1_scales[n] = pair.tile([P, PASSES, P], U8, name="h1_scales", align_bytes=64)
+            quantise(h1_grouped[n][:], h1_codes[n][:], h1_scales[n][:])
+
+        def layer2(n):
+            if no_tile(n):
+                return
+            u2[n] = psum_u2.tile([P, D_OUT], F32, name="u2")
+            for g in range(PASSES):
+                nc.tensor.matmul_mx(
+                    out=u2[n][:],
+                    lhsT=h1_codes[n][:, g, :].bitcast(FP8X4),
+                    lhsT_scale=h1_scales[n][:, g, :],
+                    rhs=w2_codes[:, g, :].bitcast(FP8X4),
+                    rhs_scale=w2_scales[:, g, :],
+                    start=(g == 0),
+                    stop=(g == PASSES - 1),
+                )
+
+        def centre2(n):
+            if no_tile(n):
+                return
+            b, i = n // BATCH, n % BATCH
+            if i == 0:
+                v2[b] = triple.tile([P, BATCH, D_OUT], F32, name="v2")
+            mean, rstd2[n] = mean_and_inverse_std([u2[n]])
+            nc.vector.scalar_tensor_tensor(
+                out=v2[b][:, i, :], in0=u2[n][:], scalar=mean, in1=gain2[:], op0=ALU.subtract, op1=ALU.mult
+            )
+
+        def scale2(n):
+            if no_tile(n):
+                return
+            rows = v2[n // BATCH][:, n % BATCH, :]
+            nc.vector.scalar_tensor_tensor(
+                out=rows, in0=rows, scalar=rstd2[n], in1=bias2[:], op0=ALU.mult, op1=ALU.add
+            )
+
+        def tanh_half2(b):
+            if no_batch(b):
+                return
+            e2[b] = pair.tile([P, BATCH * D_OUT], F32, name="e2")
+            tanh_half(e2[b][:], v2[b][:].rearrange("p i d -> p (i d)"))
+
+        def log_of_rest2(b):
+            if no_batch(b):
+                return
+            log_of_rest(e2[b][:])
+
+        def tanh_softplus2(b):
+            if no_batch(b):
+                return
+            tanh_softplus(e2[b][:])
+
+        def mish2_and_store(b):
+            if no_batch(b):
+                return
+            result = pair.tile([P, BATCH, D_OUT], F32, name="result")
+            nc.vector.tensor_tensor(
+                out=result[:].rearrange("p i d -> p (i d)"),
+                in0=v2[b][:].rearrange("p i d -> p (i d)"),
+                in1=e2[b][:],
+                op=ALU.mult,
+            )
+            rows = out[b * BATCH * P : (b + 1) * BATCH * P, :]
+            nc.sync.dma_start(out=rows.rearrange("(i p) d -> p i d", p=P), in_=result[:])
+
+        transpose_x(0)
+        for s in range(N_BATCH + 6):
+            load_x(s + 1)
+            for i in range(BATCH):
+                q = s * BATCH + i
+                mish1(q - 3 * BATCH - 1)
+                transpose_h1(q - 4 * BATCH + 1)
+                tanh_softplus1(q - 3 * BATCH)
+                tanh_half1(q - 2 * BATCH)
+                regroup_h1(q - 4 * BATCH)
+                regroup_x(q)
+                transpose_x(q + 1)
+                centre2(q - 4 * BATCH - 2)
+                centre1(q - BATCH)
+                layer1(q - BATCH + 2)
+                quantise_x(q - 1)
+                quantise_h1(q - 4 * BATCH - 1)
+                layer2(q - 4 * BATCH - 1)
+                scale1(q - BATCH)
+                scale2(q - 4 * BATCH - 2)
+            tanh_softplus2(s - 6)
+            tanh_half2(s - 5)
+            for i in range(BATCH):
+                log_of_rest1((s - 2) * BATCH + i)
+            log_of_rest2(s - 5)
+            mish2_and_store(s - 6)

@@ -253,7 +253,7 @@ def tile_autoencoder_pa_t_kernel(
                 return
             b, i = n // BATCH, n % BATCH
             h1[n] = quad.tile([P, D_HID], BF16, name="h1")
-            nc.vector.tensor_tensor(
+            nc.gpsimd.tensor_tensor(
                 out=h1[n][:],
                 in0=v1[b][:, i].rearrange("p h t m -> p (h t m)"),
                 in1=e1[b][:, i, :],
@@ -271,7 +271,7 @@ def tile_autoencoder_pa_t_kernel(
             if no_tile(n):
                 return
             h1_grouped[n] = quad.tile([P, PASSES, P, PACK], BF16, name="h1_grouped", align_bytes=64)
-            nc.scalar.copy(
+            nc.vector.tensor_copy(
                 out=h1_grouped[n][:], in_=h1_t[n][:].rearrange("p (g t) k -> p g k t", t=PACK)
             )
 
@@ -302,7 +302,7 @@ def tile_autoencoder_pa_t_kernel(
                 return
             b, i = n // BATCH, n % BATCH
             if i == 0:
-                v2[b] = triple.tile([P, BATCH, D_OUT], F32, name="v2")
+                v2[b] = quad.tile([P, BATCH, D_OUT], F32, name="v2")
             mean, rstd2[n] = mean_and_inverse_std([u2[n]])
             nc.vector.scalar_tensor_tensor(
                 out=v2[b][:, i, :], in0=u2[n][:], scalar=mean, in1=gain2[:], op0=ALU.subtract, op1=ALU.mult
@@ -336,7 +336,7 @@ def tile_autoencoder_pa_t_kernel(
             if no_batch(b):
                 return
             result = pair.tile([P, BATCH, D_OUT], F32, name="result")
-            nc.vector.tensor_tensor(
+            nc.gpsimd.tensor_tensor(
                 out=result[:].rearrange("p i d -> p (i d)"),
                 in0=v2[b][:].rearrange("p i d -> p (i d)"),
                 in1=e2[b][:],
@@ -350,21 +350,22 @@ def tile_autoencoder_pa_t_kernel(
             load_x(s + 1)
             for i in range(BATCH):
                 q = s * BATCH + i
-                mish1(q - 3 * BATCH - 1)
-                transpose_h1(q - 4 * BATCH + 1)
+                y = q - 3 * BATCH - 2
+                transpose_h1(y)
                 tanh_softplus1(q - 3 * BATCH)
                 tanh_half1(q - 2 * BATCH)
-                regroup_h1(q - 4 * BATCH)
                 regroup_x(q)
                 transpose_x(q + 1)
-                centre2(q - 4 * BATCH - 2)
+                regroup_h1(y - 1)
+                centre2(y - 3)
                 centre1(q - BATCH)
                 layer1(q - BATCH + 2)
+                mish1(q - 3 * BATCH)
                 quantise_x(q - 1)
-                quantise_h1(q - 4 * BATCH - 1)
-                layer2(q - 4 * BATCH - 1)
-                scale1(q - BATCH)
-                scale2(q - 4 * BATCH - 2)
+                quantise_h1(y - 2)
+                layer2(y - 2)
+                scale1(q - BATCH - 1)
+                scale2(y - 4)
             tanh_softplus2(s - 6)
             tanh_half2(s - 5)
             for i in range(BATCH):

@@ -253,7 +253,7 @@ def tile_autoencoder_pa_t_kernel(
                 return
             b, i = n // BATCH, n % BATCH
             h1[n] = quad.tile([P, D_HID], BF16, name="h1")
-            nc.gpsimd.tensor_tensor(
+            nc.vector.tensor_tensor(
                 out=h1[n][:],
                 in0=v1[b][:, i].rearrange("p h t m -> p (h t m)"),
                 in1=e1[b][:, i, :],
@@ -271,7 +271,7 @@ def tile_autoencoder_pa_t_kernel(
             if no_tile(n):
                 return
             h1_grouped[n] = quad.tile([P, PASSES, P, PACK], BF16, name="h1_grouped", align_bytes=64)
-            nc.vector.tensor_copy(
+            nc.scalar.copy(
                 out=h1_grouped[n][:], in_=h1_t[n][:].rearrange("p (g t) k -> p g k t", t=PACK)
             )
 
@@ -336,7 +336,7 @@ def tile_autoencoder_pa_t_kernel(
             if no_batch(b):
                 return
             result = pair.tile([P, BATCH, D_OUT], F32, name="result")
-            nc.gpsimd.tensor_tensor(
+            nc.vector.tensor_tensor(
                 out=result[:].rearrange("p i d -> p (i d)"),
                 in0=v2[b][:].rearrange("p i d -> p (i d)"),
                 in1=e2[b][:],
@@ -350,22 +350,22 @@ def tile_autoencoder_pa_t_kernel(
             load_x(s + 1)
             for i in range(BATCH):
                 q = s * BATCH + i
-                y = q - 3 * BATCH - 2
-                transpose_h1(y)
+                m = q - 3 * BATCH - 1
+                mish1(m)
+                transpose_h1(m - 1)
                 tanh_softplus1(q - 3 * BATCH)
                 tanh_half1(q - 2 * BATCH)
+                regroup_h1(m - 2)
                 regroup_x(q)
                 transpose_x(q + 1)
-                regroup_h1(y - 1)
-                centre2(y - 3)
+                centre2(m - 4)
                 centre1(q - BATCH)
                 layer1(q - BATCH + 2)
-                mish1(q - 3 * BATCH)
                 quantise_x(q - 1)
-                quantise_h1(y - 2)
-                layer2(y - 2)
+                quantise_h1(m - 3)
+                layer2(m - 3)
                 scale1(q - BATCH - 1)
-                scale2(y - 4)
+                scale2(m - 5)
             tanh_softplus2(s - 6)
             tanh_half2(s - 5)
             for i in range(BATCH):

@@ -20,8 +20,14 @@ WORDS = K_PASS // 2
 PASSES = D_IN // K_PASS
 HALVES = D_HID // K_PASS
 N_TILES = TOKENS // P
-BATCH = 4
-N_BATCH = N_TILES // BATCH
+BATCHES = [4, 4, 4, 4, 4, 4, 4, 4]
+LAG = 2
+RATE = 3
+GROUP2 = 2
+X_AHEAD = 4
+X_BUFS = 8
+V_BUFS = 14
+E_BUFS = 10
 EPS = 1e-5
 STATS = 6
 
@@ -36,8 +42,13 @@ def tile_autoencoder_pa_t_kernel(
         const = stack.enter_context(tc.tile_pool(name="const", bufs=1))
         pair = stack.enter_context(tc.tile_pool(name="pair", bufs=2))
         triple = stack.enter_context(tc.tile_pool(name="triple", bufs=3))
-        quad = stack.enter_context(tc.tile_pool(name="quad", bufs=BATCH))
-        small = stack.enter_context(tc.tile_pool(name="small", bufs=4))
+        v2pool = stack.enter_context(tc.tile_pool(name="v2pool", bufs=8))
+        e2pool = stack.enter_context(tc.tile_pool(name="e2pool", bufs=6))
+        xgpool = stack.enter_context(tc.tile_pool(name="xgpool", bufs=5))
+        xpool = stack.enter_context(tc.tile_pool(name="xpool", bufs=X_BUFS))
+        vpool = stack.enter_context(tc.tile_pool(name="vpool", bufs=V_BUFS))
+        epool = stack.enter_context(tc.tile_pool(name="epool", bufs=E_BUFS))
+        small = stack.enter_context(tc.tile_pool(name="small", bufs=6))
         psum_u1 = stack.enter_context(tc.psum_pool(name="psum_u1", bufs=2 * HALVES))
         psum_ht = stack.enter_context(tc.psum_pool(name="psum_ht", bufs=2))
         psum_xt = stack.enter_context(tc.psum_pool(name="psum_xt", bufs=1))
@@ -69,16 +80,15 @@ def tile_autoencoder_pa_t_kernel(
 
         x_rows = {}
 
-        def load_x(b):
-            if b >= N_BATCH:
+        def load_x(n):
+            if not 0 <= n < N_TILES:
                 return
-            x_rows[b] = pair.tile([P, BATCH, D_IN], BF16, name="x_rows")
-            for i in range(BATCH):
-                first = (b * BATCH + i) * P
-                nc.sync.dma_start(out=x_rows[b][:, i, :], in_=x[first : first + P, :])
+            x_rows[n] = xpool.tile([P, D_IN], BF16, name="x_rows")
+            nc.sync.dma_start(out=x_rows[n][:], in_=x[n * P : (n + 1) * P, :])
 
         load_scales(w1_scales, W1_scales)
-        load_x(0)
+        for n in range(X_AHEAD):
+            load_x(n)
         load_codes(w1_codes, W1_words)
         load_scales(w2_scales, W2_scales)
         load_codes(w2_codes, W2_words)
@@ -112,34 +122,44 @@ def tile_autoencoder_pa_t_kernel(
                 out=spread, in0=raw, scalar1=1.0, scalar2=0.0, op0=ALU.mult, op1=ALU.add
             )
 
-        def no_tile(n):
-            return n < 0 or n >= N_TILES
-
-        def no_batch(b):
-            return b < 0 or b >= N_BATCH
+        passes = []
+        first = 0
+        last_batch = []
+        for size in BATCHES:
+            batch = list(range(first, first + size))
+            passes += [("softplus", n) for n in last_batch]
+            passes.append(("tanh2", 0))
+            passes += [("half", n) for n in batch]
+            passes += [("log", n) for n in batch]
+            passes.append(("log2", 0))
+            last_batch = batch
+            first += size
+        passes += [("softplus", n) for n in last_batch]
+        passes += [("tanh2", 0), ("log2", 0), ("rest2", 0), ("tanh2", 0), ("log2", 0), ("tanh2", 0)]
 
         x_t, x_grouped, x_codes, x_scales = {}, {}, {}, {}
-        u1, rstd1, v1, e1 = {}, {}, {}, {}
+        u1, rstd1, mean1, stats1, v1, e1 = {}, {}, {}, {}, {}, {}
         h1, h1_t, h1_grouped, h1_codes, h1_scales = {}, {}, {}, {}, {}
-        u2, rstd2, v2, e2 = {}, {}, {}, {}
+        u2, rstd2, mean2, stats2, v2, e2 = {}, {}, {}, {}, {}, {}
+
+        def tile_ok(n):
+            return n is not None and 0 <= n < N_TILES
 
         def transpose_x(n):
-            if no_tile(n):
+            if not tile_ok(n):
                 return
-            words = x_rows[n // BATCH][:, n % BATCH, :].bitcast(F32)
+            words = x_rows[n][:].bitcast(F32)
             x_t[n] = psum_xt.tile([P, PASSES, 2, P], F32, name="x_t")
             for g in range(PASSES):
                 for u in range(2):
                     nc.tensor.transpose(
-                        x_t[n][:, g, u, :],
-                        words[:, g * WORDS + u : (g + 1) * WORDS : 2],
-                        ident_f32[:],
+                        x_t[n][:, g, u, :], words[:, g * WORDS + u : (g + 1) * WORDS : 2], ident_f32[:]
                     )
 
         def regroup_x(n):
-            if no_tile(n):
+            if not tile_ok(n):
                 return
-            x_grouped[n] = quad.tile([P, PASSES, P, PACK], BF16, name="x_grouped", align_bytes=64)
+            x_grouped[n] = xgpool.tile([P, PASSES, P, PACK], BF16, name="x_grouped", align_bytes=64)
             nc.scalar.copy(
                 out=x_grouped[n][:].bitcast(F32), in_=x_t[n][:].rearrange("p g u k -> p g k u")
             )
@@ -152,66 +172,67 @@ def tile_autoencoder_pa_t_kernel(
             )
 
         def quantise_x(n):
-            if no_tile(n):
+            if not tile_ok(n):
                 return
-            b, i = n // BATCH, n % BATCH
-            if i == 0:
-                x_codes[b] = pair.tile([P, BATCH, PASSES, P], U32, name="x_codes", align_bytes=64)
-                x_scales[b] = pair.tile([P, BATCH, PASSES, P], U8, name="x_scales", align_bytes=64)
-            quantise(x_grouped[n][:], x_codes[b][:, i], x_scales[b][:, i])
+            x_codes[n] = triple.tile([P, PASSES, P], U32, name="x_codes", align_bytes=64)
+            x_scales[n] = triple.tile([P, PASSES, P], U8, name="x_scales", align_bytes=64)
+            quantise(x_grouped[n][:], x_codes[n][:], x_scales[n][:])
 
         def layer1(n):
-            if no_tile(n):
+            if not tile_ok(n):
                 return
-            b, i = n // BATCH, n % BATCH
             for h in range(HALVES):
                 u1[n, h] = psum_u1.tile([P, K_PASS], F32, name="u1")
                 for g in range(PASSES):
                     nc.tensor.matmul_mx(
                         out=u1[n, h][:],
-                        lhsT=x_codes[b][:, i, g, :].bitcast(FP8X4),
-                        lhsT_scale=x_scales[b][:, i, g, :],
+                        lhsT=x_codes[n][:, g, :].bitcast(FP8X4),
+                        lhsT_scale=x_scales[n][:, g, :],
                         rhs=w1_codes[:, g, PACK * K_PASS * h : PACK * K_PASS * (h + 1)].bitcast(FP8X4),
                         rhs_scale=w1_scales[:, g, K_PASS * h : K_PASS * (h + 1)],
                         start=(g == 0),
                         stop=(g == PASSES - 1),
                     )
 
-        def mean_and_inverse_std(banks):
-            stats = small.tile([P, len(banks), STATS], F32, name="stats")
-            for j, bank in enumerate(banks):
-                nc.vector.bn_stats(out=stats[:, j, :], in_=bank[:])
-            mean_var = small.tile([P, 2], F32, name="mean_var")
-            nc.vector.bn_aggr(out=mean_var[:], in_=stats[:].rearrange("p j s -> p (j s)"))
-            shifted = small.tile([P, 1], F32, name="shifted")
-            nc.gpsimd.tensor_scalar(
-                out=shifted[:], in0=mean_var[:, 1:2], scalar1=EPS, scalar2=1.0, op0=ALU.add, op1=ALU.mult
-            )
-            rstd = small.tile([P, 1], F32, name="rstd")
-            nc.gpsimd.tensor_tensor(out=rstd[:], in0=shifted[:], in1=minus_half[:], op=ALU.pow)
-            return mean_var[:, 0:1], rstd[:, 0:1]
-
-        def centre1(n):
-            if no_tile(n):
+        def statistics1(n):
+            if not tile_ok(n):
                 return
-            b, i = n // BATCH, n % BATCH
-            if i == 0:
-                v1[b] = triple.tile([P, BATCH, HALVES, PACK, P], F32, name="v1")
-            mean, rstd1[n] = mean_and_inverse_std([u1[n, h] for h in range(HALVES)])
+            stats1[n] = small.tile([P, HALVES, STATS], F32, name="stats1")
             for h in range(HALVES):
-                nc.vector.scalar_tensor_tensor(
-                    out=v1[b][:, i, h],
-                    in0=u1[n, h][:].rearrange("p (m t) -> p t m", t=PACK),
-                    scalar=mean,
-                    in1=gain1[:, h],
-                    op0=ALU.subtract,
-                    op1=ALU.mult,
-                )
+                nc.vector.bn_stats(out=stats1[n][:, h, :], in_=u1[n, h][:])
+
+        def mean_and_std1(n):
+            if not tile_ok(n):
+                return
+            mv = small.tile([P, 2], F32, name="mean_var1")
+            nc.vector.bn_aggr(out=mv[:], in_=stats1[n][:].rearrange("p j s -> p (j s)"))
+            mean1[n], rstd1[n] = mv[:, 0:1], inverse_std(mv[:, 1:2], "1")
+
+        def inverse_std(var, which):
+            shifted = small.tile([P, 1], F32, name="shifted" + which)
+            nc.gpsimd.tensor_scalar(out=shifted[:], in0=var, scalar1=EPS, scalar2=1.0, op0=ALU.add, op1=ALU.mult)
+            rstd = small.tile([P, 1], F32, name="rstd" + which)
+            nc.gpsimd.tensor_tensor(out=rstd[:], in0=shifted[:], in1=minus_half[:], op=ALU.pow)
+            return rstd[:, 0:1]
+
+        def centre1(n, h):
+            if not tile_ok(n):
+                return
+            if h == 0:
+                v1[n] = vpool.tile([P, HALVES, PACK, P], F32, name="v1")
+            nc.vector.scalar_tensor_tensor(
+                out=v1[n][:, h],
+                in0=u1[n, h][:].rearrange("p (m t) -> p t m", t=PACK),
+                scalar=mean1[n],
+                in1=gain1[:, h],
+                op0=ALU.subtract,
+                op1=ALU.mult,
+            )
 
         def scale1(n):
-            if no_tile(n):
+            if not tile_ok(n):
                 return
-            rows = v1[n // BATCH][:, n % BATCH].rearrange("p h t m -> p (h t m)")
+            rows = v1[n][:].rearrange("p h t m -> p (h t m)")
             nc.vector.scalar_tensor_tensor(
                 out=rows,
                 in0=rows,
@@ -220,6 +241,7 @@ def tile_autoencoder_pa_t_kernel(
                 op0=ALU.mult,
                 op1=ALU.add,
             )
+            scaled1.append(n)
 
         def tanh_half(e, v):
             nc.scalar.activation(out=e, in_=v, func=ACT.Tanh, scale=0.5)
@@ -231,59 +253,43 @@ def tile_autoencoder_pa_t_kernel(
             nc.scalar.activation(out=e, in_=e, func=ACT.Tanh, scale=-1.0)
 
         def tanh_half1(n):
-            if no_tile(n):
+            if not tile_ok(n):
                 return
-            b, i = n // BATCH, n % BATCH
-            if i == 0:
-                e1[b] = pair.tile([P, BATCH, D_HID], F32, name="e1")
-            tanh_half(e1[b][:, i, :], v1[b][:, i].rearrange("p h t m -> p (h t m)"))
+            e1[n] = epool.tile([P, D_HID], F32, name="e1")
+            tanh_half(e1[n][:], v1[n][:].rearrange("p h t m -> p (h t m)"))
 
-        def log_of_rest1(n):
-            if no_tile(n):
+        def product1(n):
+            if not tile_ok(n):
                 return
-            log_of_rest(e1[n // BATCH][:, n % BATCH, :])
-
-        def tanh_softplus1(n):
-            if no_tile(n):
-                return
-            tanh_softplus(e1[n // BATCH][:, n % BATCH, :])
-
-        def mish1(n):
-            if no_tile(n):
-                return
-            b, i = n // BATCH, n % BATCH
-            h1[n] = quad.tile([P, D_HID], BF16, name="h1")
-            nc.vector.tensor_tensor(
-                out=h1[n][:],
-                in0=v1[b][:, i].rearrange("p h t m -> p (h t m)"),
-                in1=e1[b][:, i, :],
-                op=ALU.mult,
+            h1[n] = triple.tile([P, D_HID], BF16, name="h1")
+            nc.gpsimd.tensor_tensor(
+                out=h1[n][:], in0=v1[n][:].rearrange("p h t m -> p (h t m)"), in1=e1[n][:], op=ALU.mult
             )
 
         def transpose_h1(n):
-            if no_tile(n):
+            if not tile_ok(n):
                 return
             h1_t[n] = psum_ht.tile([P, PASSES * PACK, P], BF16, name="h1_t")
             for c in range(PASSES * PACK):
                 nc.tensor.transpose(h1_t[n][:, c, :], h1[n][:, c * P : (c + 1) * P], ident_bf16[:])
 
         def regroup_h1(n):
-            if no_tile(n):
+            if not tile_ok(n):
                 return
-            h1_grouped[n] = quad.tile([P, PASSES, P, PACK], BF16, name="h1_grouped", align_bytes=64)
-            nc.scalar.copy(
+            h1_grouped[n] = triple.tile([P, PASSES, P, PACK], BF16, name="h1_grouped", align_bytes=64)
+            nc.vector.tensor_copy(
                 out=h1_grouped[n][:], in_=h1_t[n][:].rearrange("p (g t) k -> p g k t", t=PACK)
             )
 
         def quantise_h1(n):
-            if no_tile(n):
+            if not tile_ok(n):
                 return
-            h1_codes[n] = pair.tile([P, PASSES, P], U32, name="h1_codes", align_bytes=64)
-            h1_scales[n] = pair.tile([P, PASSES, P], U8, name="h1_scales", align_bytes=64)
+            h1_codes[n] = triple.tile([P, PASSES, P], U32, name="h1_codes", align_bytes=64)
+            h1_scales[n] = triple.tile([P, PASSES, P], U8, name="h1_scales", align_bytes=64)
             quantise(h1_grouped[n][:], h1_codes[n][:], h1_scales[n][:])
 
         def layer2(n):
-            if no_tile(n):
+            if not tile_ok(n):
                 return
             u2[n] = psum_u2.tile([P, D_OUT], F32, name="u2")
             for g in range(PASSES):
@@ -297,78 +303,130 @@ def tile_autoencoder_pa_t_kernel(
                     stop=(g == PASSES - 1),
                 )
 
-        def centre2(n):
-            if no_tile(n):
+        def statistics2(n):
+            if not tile_ok(n):
                 return
-            b, i = n // BATCH, n % BATCH
-            if i == 0:
-                v2[b] = quad.tile([P, BATCH, D_OUT], F32, name="v2")
-            mean, rstd2[n] = mean_and_inverse_std([u2[n]])
+            stats2[n] = small.tile([P, STATS], F32, name="stats2")
+            nc.vector.bn_stats(out=stats2[n][:], in_=u2[n][:])
+
+        def mean_and_std2(n):
+            if not tile_ok(n):
+                return
+            mv = small.tile([P, 2], F32, name="mean_var2")
+            nc.vector.bn_aggr(out=mv[:], in_=stats2[n][:])
+            mean2[n], rstd2[n] = mv[:, 0:1], inverse_std(mv[:, 1:2], "2")
+
+        def centre2(n):
+            if not tile_ok(n):
+                return
+            if n % GROUP2 == 0:
+                v2[n // GROUP2] = v2pool.tile([P, GROUP2, D_OUT], F32, name="v2")
             nc.vector.scalar_tensor_tensor(
-                out=v2[b][:, i, :], in0=u2[n][:], scalar=mean, in1=gain2[:], op0=ALU.subtract, op1=ALU.mult
+                out=v2[n // GROUP2][:, n % GROUP2, :],
+                in0=u2[n][:],
+                scalar=mean2[n],
+                in1=gain2[:],
+                op0=ALU.subtract,
+                op1=ALU.mult,
             )
 
         def scale2(n):
-            if no_tile(n):
+            if not tile_ok(n):
                 return
-            rows = v2[n // BATCH][:, n % BATCH, :]
+            rows = v2[n // GROUP2][:, n % GROUP2, :]
             nc.vector.scalar_tensor_tensor(
                 out=rows, in0=rows, scalar=rstd2[n], in1=bias2[:], op0=ALU.mult, op1=ALU.add
             )
+            if n % GROUP2 == GROUP2 - 1:
+                scaled2.append(n // GROUP2)
 
-        def tanh_half2(b):
-            if no_batch(b):
-                return
-            e2[b] = pair.tile([P, BATCH * D_OUT], F32, name="e2")
-            tanh_half(e2[b][:], v2[b][:].rearrange("p i d -> p (i d)"))
+        def flat2(tile2):
+            return tile2[:].rearrange("p i d -> p (i d)")
 
-        def log_of_rest2(b):
-            if no_batch(b):
-                return
-            log_of_rest(e2[b][:])
-
-        def tanh_softplus2(b):
-            if no_batch(b):
-                return
-            tanh_softplus(e2[b][:])
-
-        def mish2_and_store(b):
-            if no_batch(b):
-                return
-            result = pair.tile([P, BATCH, D_OUT], F32, name="result")
-            nc.vector.tensor_tensor(
-                out=result[:].rearrange("p i d -> p (i d)"),
-                in0=v2[b][:].rearrange("p i d -> p (i d)"),
-                in1=e2[b][:],
-                op=ALU.mult,
-            )
-            rows = out[b * BATCH * P : (b + 1) * BATCH * P, :]
+        def product2_and_store(e):
+            result = pair.tile([P, GROUP2, D_OUT], F32, name="result")
+            nc.vector.tensor_tensor(out=flat2(result), in0=flat2(v2[e]), in1=flat2(e2[e]), op=ALU.mult)
+            rows = out[e * GROUP2 * P : (e + 1) * GROUP2 * P, :]
             nc.sync.dma_start(out=rows.rearrange("(i p) d -> p i d", p=P), in_=result[:])
 
+        scaled1, scaled2 = [], []
+        waiting2, logged2, finished2 = [], [], []
+        softplus_in_slot, product_slot, stored2 = {}, {}, []
+        place = {"next": 0}
+
+        def next_pass(q):
+            if place["next"] == len(passes):
+                return 0
+            kind, n = passes[place["next"]]
+            if kind == "half":
+                if n not in scaled1:
+                    return 0
+                tanh_half1(n)
+            if kind == "log":
+                log_of_rest(e1[n][:])
+            if kind == "softplus":
+                tanh_softplus(e1[n][:])
+                softplus_in_slot[n] = q
+            if kind == "rest2" and len(stored2) + len(scaled2) + len(logged2) + len(waiting2) + len(finished2) < N_TILES // GROUP2:
+                return 0
+            if kind == "tanh2":
+                for e in logged2:
+                    tanh_softplus(flat2(e2[e]))
+                    finished2.append(e)
+                logged2.clear()
+                for e in scaled2:
+                    e2[e] = e2pool.tile([P, GROUP2, D_OUT], F32, name="e2")
+                    tanh_half(flat2(e2[e]), flat2(v2[e]))
+                    waiting2.append(e)
+                scaled2.clear()
+            if kind == "log2":
+                for e in waiting2:
+                    log_of_rest(flat2(e2[e]))
+                    logged2.append(e)
+                waiting2.clear()
+            place["next"] += 1
+            return 1 if kind in ("half", "log", "softplus") else 0.01
+
         transpose_x(0)
-        for s in range(N_BATCH + 6):
-            load_x(s + 1)
-            for i in range(BATCH):
-                q = s * BATCH + i
-                m = q - 3 * BATCH - 1
-                mish1(m)
-                transpose_h1(m - 1)
-                tanh_softplus1(q - 3 * BATCH)
-                tanh_half1(q - 2 * BATCH)
-                regroup_h1(m - 2)
-                regroup_x(q)
-                transpose_x(q + 1)
-                centre2(m - 4)
-                centre1(q - BATCH)
-                layer1(q - BATCH + 2)
-                quantise_x(q - 1)
-                quantise_h1(m - 3)
-                layer2(m - 3)
-                scale1(q - BATCH - 1)
-                scale2(m - 5)
-            tanh_softplus2(s - 6)
-            tanh_half2(s - 5)
-            for i in range(BATCH):
-                log_of_rest1((s - 2) * BATCH + i)
-            log_of_rest2(s - 5)
-            mish2_and_store(s - 6)
+        q = -3
+        while len(stored2) < N_TILES // GROUP2:
+            q += 1
+            n = q - 3
+            made = len(product_slot)
+            if made in softplus_in_slot and softplus_in_slot[made] + LAG <= q:
+                product_slot[made] = q
+            m0, m1, m2, m3 = ([k for k in product_slot if product_slot[k] == q - j] for j in range(4))
+            m0, m1, m2, m3 = ((m[0] if m else None) for m in (m0, m1, m2, m3))
+            load_x(n + 5 + X_AHEAD)
+            def passes_up_to(share):
+                while place["done"] < share:
+                    weight = next_pass(q)
+                    if weight == 0:
+                        break
+                    place["done"] += weight
+
+            place["done"] = 0
+            passes_up_to(1)
+            regroup_x(n + 5)
+            passes_up_to(RATE)
+            transpose_x(n + 6)
+            product1(m0)
+            transpose_h1(m1)
+            centre1(n + 1, 0)
+            centre1(n + 1, 1)
+            statistics2(m2)
+            statistics1(n + 2)
+            mean_and_std2(m2)
+            regroup_h1(m1)
+            centre2(m2)
+            quantise_x(n + 3)
+            layer1(n + 3)
+            scale1(n)
+            scale2(m3)
+            for e in finished2:
+                product2_and_store(e)
+                stored2.append(e)
+            finished2.clear()
+            quantise_h1(m1)
+            layer2(m1)
+            mean_and_std1(n + 2)

@@ -99,7 +99,7 @@ def tile_autoencoder_pa_t_kernel(
         make_identity(nc, ident_bf16[:])
         half = const.tile([P, 1], F32)
         nc.vector.memset(half[:], 0.5)
-        minus_half = const.tile([P, 1], F32)
+        minus_half = const.tile([P, 2], F32)
         nc.vector.memset(minus_half[:], -0.5)
 
         raw_g1 = const.tile([P, D_HID], BF16)
@@ -201,19 +201,39 @@ def tile_autoencoder_pa_t_kernel(
             for h in range(HALVES):
                 nc.vector.bn_stats(out=stats1[n][:, h, :], in_=u1[n, h][:])
 
-        def mean_and_std1(n):
+        def mean1_of(n, mean_var):
             if not tile_ok(n):
                 return
-            mv = small.tile([P, 2], F32, name="mean_var1")
-            nc.vector.bn_aggr(out=mv[:], in_=stats1[n][:].rearrange("p j s -> p (j s)"))
-            mean1[n], rstd1[n] = mv[:, 0:1], inverse_std(mv[:, 1:2], "1")
+            nc.vector.bn_aggr(out=mean_var[:, 0, :], in_=stats1[n][:].rearrange("p j s -> p (j s)"))
+            mean1[n] = mean_var[:, 0, 0:1]
 
-        def inverse_std(var, which):
-            shifted = small.tile([P, 1], F32, name="shifted" + which)
-            nc.gpsimd.tensor_scalar(out=shifted[:], in0=var, scalar1=EPS, scalar2=1.0, op0=ALU.add, op1=ALU.mult)
-            rstd = small.tile([P, 1], F32, name="rstd" + which)
-            nc.gpsimd.tensor_tensor(out=rstd[:], in0=shifted[:], in1=minus_half[:], op=ALU.pow)
-            return rstd[:, 0:1]
+        def mean2_of(n, mean_var):
+            if not tile_ok(n):
+                return
+            nc.vector.bn_aggr(out=mean_var[:, 1, :], in_=stats2[n][:])
+            mean2[n] = mean_var[:, 1, 0:1]
+
+        def inverse_std(n, k, mean_var):
+            first, last = (0 if tile_ok(n) else 1), (2 if tile_ok(k) else 1)
+            if first == last:
+                return
+            shifted = small.tile([P, 2], F32, name="shifted")
+            rstd = small.tile([P, 2], F32, name="rstd")
+            nc.gpsimd.tensor_scalar(
+                out=shifted[:, first:last],
+                in0=mean_var[:, first:last, 1],
+                scalar1=EPS,
+                scalar2=1.0,
+                op0=ALU.add,
+                op1=ALU.mult,
+            )
+            nc.gpsimd.tensor_tensor(
+                out=rstd[:, first:last], in0=shifted[:, first:last], in1=minus_half[:, first:last], op=ALU.pow
+            )
+            if tile_ok(n):
+                rstd1[n] = rstd[:, 0:1]
+            if tile_ok(k):
+                rstd2[k] = rstd[:, 1:2]
 
         def centre1(n, h):
             if not tile_ok(n):
@@ -309,13 +329,6 @@ def tile_autoencoder_pa_t_kernel(
             stats2[n] = small.tile([P, STATS], F32, name="stats2")
             nc.vector.bn_stats(out=stats2[n][:], in_=u2[n][:])
 
-        def mean_and_std2(n):
-            if not tile_ok(n):
-                return
-            mv = small.tile([P, 2], F32, name="mean_var2")
-            nc.vector.bn_aggr(out=mv[:], in_=stats2[n][:])
-            mean2[n], rstd2[n] = mv[:, 0:1], inverse_std(mv[:, 1:2], "2")
-
         def centre2(n):
             if not tile_ok(n):
                 return
@@ -410,13 +423,14 @@ def tile_autoencoder_pa_t_kernel(
             regroup_x(n + 5)
             passes_up_to(RATE)
             transpose_x(n + 6)
+            mean_var = small.tile([P, 2, 2], F32, name="mean_var")
             product1(m0)
             transpose_h1(m1)
             centre1(n + 1, 0)
             centre1(n + 1, 1)
             statistics2(m2)
             statistics1(n + 2)
-            mean_and_std2(m2)
+            mean2_of(m2, mean_var)
             regroup_h1(m1)
             centre2(m2)
             quantise_x(n + 3)
@@ -429,4 +443,5 @@ def tile_autoencoder_pa_t_kernel(
             finished2.clear()
             quantise_h1(m1)
             layer2(m1)
-            mean_and_std1(n + 2)
+            mean1_of(n + 2, mean_var)
+            inverse_std(n + 2, m2, mean_var)

@@ -57,8 +57,18 @@ def tile_autoencoder_pa_t_kernel(
 
         w1_scales = const.tile([P, PASSES, D_HID], U8, align_bytes=64)
         w2_scales = const.tile([P, PASSES, D_OUT], U8, align_bytes=64)
-        nc.vector.memset(w1_scales[:].bitcast(I32), 0)
+        nc.gpsimd.memset(w1_scales[:].bitcast(I32), 0)
+        rows1 = const.tile([P, 2, D_HID], BF16)
+        rows2 = const.tile([P, 2, D_OUT], BF16)
+        nc.vector.memset(rows1[:], 0.0)
+        nc.vector.memset(rows2[:], 0.0)
+        for j, row in enumerate((g1, b1)):
+            nc.scalar.dma_start(out=rows1[0:1, j, :], in_=row.unsqueeze(0))
+        for j, row in enumerate((g2, b2)):
+            nc.scalar.dma_start(out=rows2[0:1, j, :], in_=row.unsqueeze(0))
         nc.vector.memset(w2_scales[:].bitcast(I32), 0)
+        ones = const.tile([P, P], BF16)
+        nc.vector.memset(ones[:], 1.0)
         w1_codes = const.tile([P, PASSES, PACK * D_HID], U8, align_bytes=64)
         w2_codes = const.tile([P, PASSES, PACK * D_OUT], U8, align_bytes=64)
 
@@ -86,41 +96,42 @@ def tile_autoencoder_pa_t_kernel(
             x_rows[n] = xpool.tile([P, D_IN], BF16, name="x_rows")
             nc.sync.dma_start(out=x_rows[n][:], in_=x[n * P : (n + 1) * P, :])
 
+        load_x(0)
         load_scales(w1_scales, W1_scales)
-        for n in range(X_AHEAD):
-            load_x(n)
-        load_codes(w1_codes, W1_words)
+        for h in range(HALVES):
+            columns = slice(h * K_PASS, (h + 1) * K_PASS)
+            for g in range(PASSES):
+                nc.sync.dma_start(
+                    out=w1_codes[:, g, PACK * h * K_PASS : PACK * (h + 1) * K_PASS].bitcast(I32),
+                    in_=W1_words[g, :, columns, :].rearrange("p n t -> p (n t)").bitcast(I32),
+                )
+            load_x(h + 1)
+        load_x(3)
         load_scales(w2_scales, W2_scales)
         load_codes(w2_codes, W2_words)
 
         ident_f32 = const.tile([P, P], F32)
         make_identity(nc, ident_f32[:])
-        ident_bf16 = const.tile([P, P], BF16)
-        make_identity(nc, ident_bf16[:])
         half = const.tile([P, 1], F32)
         nc.vector.memset(half[:], 0.5)
         minus_half = const.tile([P, 2], F32)
         nc.vector.memset(minus_half[:], -0.5)
 
-        raw_g1 = const.tile([P, D_HID], BF16)
-        raw_b1 = const.tile([P, D_HID], BF16)
-        raw_g2 = const.tile([P, D_OUT], BF16)
-        raw_b2 = const.tile([P, D_OUT], BF16)
-        for raw, vector in ((raw_g1, g1), (raw_b1, b1), (raw_g2, g2), (raw_b2, b2)):
-            nc.scalar.dma_start(out=raw[:], in_=vector.partition_broadcast(P))
-        gain1 = const.tile([P, HALVES, PACK, P], F32)
-        bias1 = const.tile([P, HALVES, PACK, P], F32)
-        gain2 = const.tile([P, D_OUT], F32)
-        bias2 = const.tile([P, D_OUT], F32)
-        for spread, raw in (
-            (gain1[:], raw_g1[:].rearrange("p (h m t) -> p h t m", h=HALVES, t=PACK)),
-            (bias1[:], raw_b1[:].rearrange("p (h m t) -> p h t m", h=HALVES, t=PACK)),
-            (gain2[:], raw_g2[:]),
-            (bias2[:], raw_b2[:]),
-        ):
-            nc.gpsimd.tensor_scalar(
-                out=spread, in0=raw, scalar1=1.0, scalar2=0.0, op0=ALU.mult, op1=ALU.add
-            )
+        gains = const.tile([P, 2, D_HID], F32)
+        gains2 = const.tile([P, 2, D_OUT], F32)
+
+        def spread_rows(j):
+            for rows, wide in (
+                ((rows2[:].rearrange("p j d -> p (j d)"), gains2[:].rearrange("p j d -> p (j d)")),)
+                if j == 2
+                else tuple(
+                    (rows1[:, j, h * K_PASS : (h + 1) * K_PASS], gains[:, j, h * K_PASS : (h + 1) * K_PASS])
+                    for h in range(HALVES)
+                )
+            ):
+                spread = psum_ht.tile([P, K_PASS], F32, name="h1_t")
+                nc.tensor.matmul(spread[:], lhsT=ones[:], rhs=rows, start=True, stop=True)
+                nc.scalar.copy(out=wide, in_=spread[:])
 
         passes = []
         first = 0
@@ -239,12 +250,12 @@ def tile_autoencoder_pa_t_kernel(
             if not tile_ok(n):
                 return
             if h == 0:
-                v1[n] = vpool.tile([P, HALVES, PACK, P], F32, name="v1")
+                v1[n] = vpool.tile([P, HALVES, K_PASS], F32, name="v1")
             nc.vector.scalar_tensor_tensor(
                 out=v1[n][:, h],
-                in0=u1[n, h][:].rearrange("p (m t) -> p t m", t=PACK),
+                in0=u1[n, h][:],
                 scalar=mean1[n],
-                in1=gain1[:, h],
+                in1=gains[:, 0, h * K_PASS : (h + 1) * K_PASS],
                 op0=ALU.subtract,
                 op1=ALU.mult,
             )
@@ -252,12 +263,12 @@ def tile_autoencoder_pa_t_kernel(
         def scale1(n):
             if not tile_ok(n):
                 return
-            rows = v1[n][:].rearrange("p h t m -> p (h t m)")
+            rows = v1[n][:].rearrange("p h m -> p (h m)")
             nc.vector.scalar_tensor_tensor(
                 out=rows,
                 in0=rows,
                 scalar=rstd1[n],
-                in1=bias1[:].rearrange("p h t m -> p (h t m)"),
+                in1=gains[:, 1, :],
                 op0=ALU.mult,
                 op1=ALU.add,
             )
@@ -276,29 +287,33 @@ def tile_autoencoder_pa_t_kernel(
             if not tile_ok(n):
                 return
             e1[n] = epool.tile([P, D_HID], F32, name="e1")
-            tanh_half(e1[n][:], v1[n][:].rearrange("p h t m -> p (h t m)"))
+            tanh_half(e1[n][:], v1[n][:].rearrange("p h m -> p (h m)"))
 
         def product1(n):
             if not tile_ok(n):
                 return
             h1[n] = triple.tile([P, D_HID], BF16, name="h1")
-            nc.gpsimd.tensor_tensor(
-                out=h1[n][:], in0=v1[n][:].rearrange("p h t m -> p (h t m)"), in1=e1[n][:], op=ALU.mult
+            nc.vector.tensor_tensor(
+                out=h1[n][:], in0=v1[n][:].rearrange("p h m -> p (h m)"), in1=e1[n][:], op=ALU.mult
             )
 
         def transpose_h1(n):
             if not tile_ok(n):
                 return
-            h1_t[n] = psum_ht.tile([P, PASSES * PACK, P], BF16, name="h1_t")
-            for c in range(PASSES * PACK):
-                nc.tensor.transpose(h1_t[n][:, c, :], h1[n][:, c * P : (c + 1) * P], ident_bf16[:])
+            words = h1[n][:].bitcast(F32)
+            h1_t[n] = psum_ht.tile([P, PASSES, 2, P], F32, name="h1_t")
+            for g in range(PASSES):
+                for u in range(2):
+                    nc.tensor.transpose(
+                        h1_t[n][:, g, u, :], words[:, g * WORDS + u : (g + 1) * WORDS : 2], ident_f32[:]
+                    )
 
         def regroup_h1(n):
             if not tile_ok(n):
                 return
             h1_grouped[n] = triple.tile([P, PASSES, P, PACK], BF16, name="h1_grouped", align_bytes=64)
-            nc.vector.tensor_copy(
-                out=h1_grouped[n][:], in_=h1_t[n][:].rearrange("p (g t) k -> p g k t", t=PACK)
+            nc.scalar.copy(
+                out=h1_grouped[n][:].bitcast(F32), in_=h1_t[n][:].rearrange("p g u k -> p g k u")
             )
 
         def quantise_h1(n):
@@ -338,7 +353,7 @@ def tile_autoencoder_pa_t_kernel(
                 out=v2[n // GROUP2][:, n % GROUP2, :],
                 in0=u2[n][:],
                 scalar=mean2[n],
-                in1=gain2[:],
+                in1=gains2[:, 0, :],
                 op0=ALU.subtract,
                 op1=ALU.mult,
             )
@@ -348,7 +363,7 @@ def tile_autoencoder_pa_t_kernel(
                 return
             rows = v2[n // GROUP2][:, n % GROUP2, :]
             nc.vector.scalar_tensor_tensor(
-                out=rows, in0=rows, scalar=rstd2[n], in1=bias2[:], op0=ALU.mult, op1=ALU.add
+                out=rows, in0=rows, scalar=rstd2[n], in1=gains2[:, 1, :], op0=ALU.mult, op1=ALU.add
             )
             if n % GROUP2 == GROUP2 - 1:
                 scaled2.append(n // GROUP2)
@@ -408,8 +423,8 @@ def tile_autoencoder_pa_t_kernel(
             made = len(product_slot)
             if made in softplus_in_slot and softplus_in_slot[made] + LAG <= q:
                 product_slot[made] = q
-            m0, m1, m2, m3 = ([k for k in product_slot if product_slot[k] == q - j] for j in range(4))
-            m0, m1, m2, m3 = ((m[0] if m else None) for m in (m0, m1, m2, m3))
+            m0, m1, m2, m3, m4 = ([k for k in product_slot if product_slot[k] == q - j] for j in range(5))
+            m0, m1, m2, m3, m4 = ((m[0] if m else None) for m in (m0, m1, m2, m3, m4))
             load_x(n + 5 + X_AHEAD)
             def passes_up_to(share):
                 while place["done"] < share:
@@ -419,29 +434,32 @@ def tile_autoencoder_pa_t_kernel(
                     place["done"] += weight
 
             place["done"] = 0
+            mean_var = small.tile([P, 2, 2], F32, name="mean_var")
             passes_up_to(1)
             regroup_x(n + 5)
+            passes_up_to(2)
+            regroup_h1(m1)
+            if 0 <= n + 5 <= 2:
+                spread_rows(n + 5)
             passes_up_to(RATE)
             transpose_x(n + 6)
-            mean_var = small.tile([P, 2, 2], F32, name="mean_var")
-            product1(m0)
-            transpose_h1(m1)
+            statistics2(m3)
             centre1(n + 1, 0)
             centre1(n + 1, 1)
-            statistics2(m2)
+            mean2_of(m3, mean_var)
+            product1(m0)
+            transpose_h1(m0)
             statistics1(n + 2)
-            mean2_of(m2, mean_var)
-            regroup_h1(m1)
-            centre2(m2)
+            centre2(m3)
             quantise_x(n + 3)
             layer1(n + 3)
             scale1(n)
-            scale2(m3)
+            scale2(m4)
+            quantise_h1(m2)
+            layer2(m2)
+            mean1_of(n + 2, mean_var)
+            inverse_std(n + 2, m3, mean_var)
             for e in finished2:
                 product2_and_store(e)
                 stored2.append(e)
             finished2.clear()
-            quantise_h1(m1)
-            layer2(m1)
-            mean1_of(n + 2, mean_var)
-            inverse_std(n + 2, m2, mean_var)

@@ -21,13 +21,16 @@ PASSES = D_IN // K_PASS
 HALVES = D_HID // K_PASS
 N_TILES = TOKENS // P
 BATCHES = [4, 4, 4, 4, 4, 4, 4, 4]
+TAIL_PAIRS = (14, 16)
+G_COLS = 0
+BEHIND = 7
 LAG = 2
 RATE = 3
 GROUP2 = 2
 X_AHEAD = 4
 X_BUFS = 8
-V_BUFS = 14
-E_BUFS = 10
+V_BUFS = 15
+E_BUFS = 12
 EPS = 1e-5
 STATS = 6
 
@@ -43,7 +46,7 @@ def tile_autoencoder_pa_t_kernel(
         pair = stack.enter_context(tc.tile_pool(name="pair", bufs=2))
         triple = stack.enter_context(tc.tile_pool(name="triple", bufs=3))
         v2pool = stack.enter_context(tc.tile_pool(name="v2pool", bufs=8))
-        e2pool = stack.enter_context(tc.tile_pool(name="e2pool", bufs=6))
+        e2pool = stack.enter_context(tc.tile_pool(name="e2pool", bufs=8))
         xgpool = stack.enter_context(tc.tile_pool(name="xgpool", bufs=5))
         xpool = stack.enter_context(tc.tile_pool(name="xpool", bufs=X_BUFS))
         vpool = stack.enter_context(tc.tile_pool(name="vpool", bufs=V_BUFS))
@@ -146,7 +149,10 @@ def tile_autoencoder_pa_t_kernel(
             last_batch = batch
             first += size
         passes += [("softplus", n) for n in last_batch]
-        passes += [("tanh2", 0), ("log2", 0), ("rest2", 0), ("tanh2", 0), ("log2", 0), ("tanh2", 0)]
+        passes += [("tanh2", 0), ("log2", 0)]
+        for pairs in TAIL_PAIRS:
+            passes += [("wait2", pairs), ("tanh2", 0), ("log2", 0)]
+        passes.append(("tanh2", 0))
 
         x_t, x_grouped, x_codes, x_scales = {}, {}, {}, {}
         u1, rstd1, mean1, stats1, v1, e1 = {}, {}, {}, {}, {}, {}
@@ -289,12 +295,16 @@ def tile_autoencoder_pa_t_kernel(
             e1[n] = epool.tile([P, D_HID], F32, name="e1")
             tanh_half(e1[n][:], v1[n][:].rearrange("p h m -> p (h m)"))
 
-        def product1(n):
+        def product1(n, engine, columns):
             if not tile_ok(n):
                 return
-            h1[n] = triple.tile([P, D_HID], BF16, name="h1")
-            nc.vector.tensor_tensor(
-                out=h1[n][:], in0=v1[n][:].rearrange("p h m -> p (h m)"), in1=e1[n][:], op=ALU.mult
+            if n not in h1:
+                h1[n] = triple.tile([P, D_HID], BF16, name="h1")
+            engine.tensor_tensor(
+                out=h1[n][:, columns],
+                in0=v1[n][:].rearrange("p h m -> p (h m)")[:, columns],
+                in1=e1[n][:, columns],
+                op=ALU.mult,
             )
 
         def transpose_h1(n):
@@ -395,7 +405,7 @@ def tile_autoencoder_pa_t_kernel(
             if kind == "softplus":
                 tanh_softplus(e1[n][:])
                 softplus_in_slot[n] = q
-            if kind == "rest2" and len(stored2) + len(scaled2) + len(logged2) + len(waiting2) + len(finished2) < N_TILES // GROUP2:
+            if kind == "wait2" and len(stored2) + len(scaled2) + len(logged2) + len(waiting2) + len(finished2) < n:
                 return 0
             if kind == "tanh2":
                 for e in logged2:
@@ -421,8 +431,9 @@ def tile_autoencoder_pa_t_kernel(
             q += 1
             n = q - 3
             made = len(product_slot)
-            if made in softplus_in_slot and softplus_in_slot[made] + LAG <= q:
-                product_slot[made] = q
+            if made < N_TILES and n >= made + BEHIND or n > N_TILES:
+                if made < N_TILES:
+                    product_slot[made] = q
             m0, m1, m2, m3, m4 = ([k for k in product_slot if product_slot[k] == q - j] for j in range(5))
             m0, m1, m2, m3, m4 = ((m[0] if m else None) for m in (m0, m1, m2, m3, m4))
             load_x(n + 5 + X_AHEAD)
@@ -441,22 +452,27 @@ def tile_autoencoder_pa_t_kernel(
             regroup_h1(m1)
             if 0 <= n + 5 <= 2:
                 spread_rows(n + 5)
+            while m0 is not None and m0 not in softplus_in_slot:
+                if next_pass(q) == 0:
+                    raise AssertionError("product before its input")
             passes_up_to(RATE)
-            transpose_x(n + 6)
-            statistics2(m3)
+            if G_COLS:
+                product1(m0, nc.gpsimd if n < N_TILES else nc.vector, slice(0, G_COLS))
             centre1(n + 1, 0)
             centre1(n + 1, 1)
-            mean2_of(m3, mean_var)
-            product1(m0)
-            transpose_h1(m0)
             statistics1(n + 2)
-            centre2(m3)
+            statistics2(m3)
+            product1(m0, nc.vector, slice(G_COLS, D_HID))
+            transpose_h1(m0)
+            mean2_of(m3, mean_var)
             quantise_x(n + 3)
             layer1(n + 3)
+            transpose_x(n + 6)
+            centre2(m3)
             scale1(n)
-            scale2(m4)
             quantise_h1(m2)
             layer2(m2)
+            scale2(m4)
             mean1_of(n + 2, mean_var)
             inverse_std(n + 2, m3, mean_var)
             for e in finished2:

@@ -22,7 +22,7 @@ HALVES = D_HID // K_PASS
 N_TILES = TOKENS // P
 BATCHES = [4, 4, 4, 4, 4, 4, 4, 4]
 TAIL_PAIRS = (14, 16)
-G_COLS = 0
+G_COLS = 512
 BEHIND = 7
 LAG = 2
 RATE = 3

@@ -22,7 +22,9 @@ HALVES = D_HID // K_PASS
 N_TILES = TOKENS // P
 BATCHES = [4, 4, 4, 4, 4, 4, 4, 4]
 TAIL_PAIRS = (14, 16)
-G_COLS = 512
+Z_EVERY = 2
+Z_WHICH = 1
+V_TOKENS = 0
 BEHIND = 7
 LAG = 2
 RATE = 3
@@ -53,7 +55,7 @@ def tile_autoencoder_pa_t_kernel(
         epool = stack.enter_context(tc.tile_pool(name="epool", bufs=E_BUFS))
         small = stack.enter_context(tc.tile_pool(name="small", bufs=6))
         psum_u1 = stack.enter_context(tc.psum_pool(name="psum_u1", bufs=2 * HALVES))
-        psum_ht = stack.enter_context(tc.psum_pool(name="psum_ht", bufs=2))
+        psum_z = stack.enter_context(tc.psum_pool(name="psum_z", bufs=HALVES))
         psum_xt = stack.enter_context(tc.psum_pool(name="psum_xt", bufs=1))
         psum_u2 = stack.enter_context(tc.psum_pool(name="psum_u2", bufs=1))
         stack.enter_context(tc.manual_schedule())
@@ -61,12 +63,13 @@ def tile_autoencoder_pa_t_kernel(
         w1_scales = const.tile([P, PASSES, D_HID], U8, align_bytes=64)
         w2_scales = const.tile([P, PASSES, D_OUT], U8, align_bytes=64)
         nc.gpsimd.memset(w1_scales[:].bitcast(I32), 0)
-        rows1 = const.tile([P, 2, D_HID], BF16)
+        raw1 = []
+        for row in (g1, b1):
+            raw = const.tile([P, HALVES, PACK], BF16, name="raw_gain1" if row is g1 else "raw_bias1")
+            nc.scalar.dma_start(out=raw[:], in_=row.rearrange("(h p t) -> p h t", h=HALVES, t=PACK))
+            raw1.append(raw)
         rows2 = const.tile([P, 2, D_OUT], BF16)
-        nc.vector.memset(rows1[:], 0.0)
         nc.vector.memset(rows2[:], 0.0)
-        for j, row in enumerate((g1, b1)):
-            nc.scalar.dma_start(out=rows1[0:1, j, :], in_=row.unsqueeze(0))
         for j, row in enumerate((g2, b2)):
             nc.scalar.dma_start(out=rows2[0:1, j, :], in_=row.unsqueeze(0))
         nc.vector.memset(w2_scales[:].bitcast(I32), 0)
@@ -120,21 +123,15 @@ def tile_autoencoder_pa_t_kernel(
         minus_half = const.tile([P, 2], F32)
         nc.vector.memset(minus_half[:], -0.5)
 
-        gains = const.tile([P, 2, D_HID], F32)
+        columns1 = const.tile([P, 2, HALVES, PACK], F32)
         gains2 = const.tile([P, 2, D_OUT], F32)
 
-        def spread_rows(j):
-            for rows, wide in (
-                ((rows2[:].rearrange("p j d -> p (j d)"), gains2[:].rearrange("p j d -> p (j d)")),)
-                if j == 2
-                else tuple(
-                    (rows1[:, j, h * K_PASS : (h + 1) * K_PASS], gains[:, j, h * K_PASS : (h + 1) * K_PASS])
-                    for h in range(HALVES)
-                )
-            ):
-                spread = psum_ht.tile([P, K_PASS], F32, name="h1_t")
-                nc.tensor.matmul(spread[:], lhsT=ones[:], rhs=rows, start=True, stop=True)
-                nc.scalar.copy(out=wide, in_=spread[:])
+        def spread_gains():
+            for j in range(2):
+                nc.vector.tensor_copy(out=columns1[:, j], in_=raw1[j][:])
+            spread = psum_z.tile([P, K_PASS], F32, name="z_t")
+            nc.tensor.matmul(spread[:], lhsT=ones[:], rhs=rows2[:].rearrange("p j d -> p (j d)"), start=True, stop=True)
+            nc.scalar.copy(out=gains2[:].rearrange("p j d -> p (j d)"), in_=spread[:])
 
         passes = []
         first = 0
@@ -155,8 +152,8 @@ def tile_autoencoder_pa_t_kernel(
         passes.append(("tanh2", 0))
 
         x_t, x_grouped, x_codes, x_scales = {}, {}, {}, {}
-        u1, rstd1, mean1, stats1, v1, e1 = {}, {}, {}, {}, {}, {}
-        h1, h1_t, h1_grouped, h1_codes, h1_scales = {}, {}, {}, {}, {}
+        u1, rstd1, mean1, shift1, stats1, z1, z_t, v1, e1 = {}, {}, {}, {}, {}, {}, {}, {}, {}
+        h1_grouped, h1_codes, h1_scales = {}, {}, {}
         u2, rstd2, mean2, stats2, v2, e2 = {}, {}, {}, {}, {}, {}
 
         def tile_ok(n):
@@ -249,35 +246,63 @@ def tile_autoencoder_pa_t_kernel(
             )
             if tile_ok(n):
                 rstd1[n] = rstd[:, 0:1]
+                if z_on_scalar(n, 1):
+                    shift = small.tile([P, 1], F32, name="shift")
+                    nc.gpsimd.tensor_scalar(
+                        out=shift[:], in0=mean_var[:, 0, 0:1], scalar1=rstd1[n], scalar2=-1.0, op0=ALU.mult, op1=ALU.mult
+                    )
+                    shift1[n] = shift[:, 0:1]
             if tile_ok(k):
                 rstd2[k] = rstd[:, 1:2]
 
-        def centre1(n, h):
-            if not tile_ok(n):
-                return
-            if h == 0:
-                v1[n] = vpool.tile([P, HALVES, K_PASS], F32, name="v1")
-            nc.vector.scalar_tensor_tensor(
-                out=v1[n][:, h],
-                in0=u1[n, h][:],
-                scalar=mean1[n],
-                in1=gains[:, 0, h * K_PASS : (h + 1) * K_PASS],
-                op0=ALU.subtract,
-                op1=ALU.mult,
-            )
+        def z_on_scalar(n, h):
+            return h == 1 and n % Z_EVERY < Z_WHICH
 
-        def scale1(n):
+        def normalise1(n, h):
             if not tile_ok(n):
                 return
-            rows = v1[n][:].rearrange("p h m -> p (h m)")
-            nc.vector.scalar_tensor_tensor(
-                out=rows,
-                in0=rows,
-                scalar=rstd1[n],
-                in1=gains[:, 1, :],
-                op0=ALU.mult,
-                op1=ALU.add,
-            )
+            if n not in z1:
+                z1[n] = pair.tile([P, HALVES, PACK, P], F32, name="z1")
+            if z_on_scalar(n, h):
+                nc.scalar.activation(
+                    out=z1[n][:, h],
+                    in_=u1[n, h][:].rearrange("p (m t) -> p t m", t=PACK),
+                    func=ACT.Identity,
+                    scale=rstd1[n],
+                    bias=shift1[n],
+                )
+            else:
+                nc.vector.tensor_scalar(
+                    out=z1[n][:, h],
+                    in0=u1[n, h][:].rearrange("p (m t) -> p t m", t=PACK),
+                    scalar1=mean1[n],
+                    scalar2=rstd1[n],
+                    op0=ALU.subtract,
+                    op1=ALU.mult,
+                )
+
+        def transpose_z(n):
+            if not tile_ok(n):
+                return
+            for h in range(HALVES):
+                z_t[n, h] = psum_z.tile([P, PACK, P], F32, name="z_t")
+                for t in range(PACK):
+                    nc.tensor.transpose(z_t[n, h][:, t, :], z1[n][:, h, t, :], ident_f32[:])
+
+        def affine1(n):
+            if not tile_ok(n):
+                return
+            v1[n] = vpool.tile([P, HALVES, PACK, P], F32, name="v1")
+            for h in range(HALVES):
+                for t in range(PACK):
+                    nc.vector.tensor_scalar(
+                        out=v1[n][:, h, t, :],
+                        in0=z_t[n, h][:, t, :],
+                        scalar1=columns1[:, 0, h, t : t + 1],
+                        scalar2=columns1[:, 1, h, t : t + 1],
+                        op0=ALU.mult,
+                        op1=ALU.add,
+                    )
             scaled1.append(n)
 
         def tanh_half(e, v):
@@ -293,37 +318,20 @@ def tile_autoencoder_pa_t_kernel(
             if not tile_ok(n):
                 return
             e1[n] = epool.tile([P, D_HID], F32, name="e1")
-            tanh_half(e1[n][:], v1[n][:].rearrange("p h m -> p (h m)"))
+            tanh_half(e1[n][:], v1[n][:].rearrange("p h t m -> p (h t m)"))
 
-        def product1(n, engine, columns):
+        def product1(n, engine, h, tokens):
             if not tile_ok(n):
                 return
-            if n not in h1:
-                h1[n] = triple.tile([P, D_HID], BF16, name="h1")
+            if n not in h1_grouped:
+                h1_grouped[n] = triple.tile([P, PASSES, P, PACK], BF16, name="h1_grouped", align_bytes=64)
             engine.tensor_tensor(
-                out=h1[n][:, columns],
-                in0=v1[n][:].rearrange("p h m -> p (h m)")[:, columns],
-                in1=e1[n][:, columns],
+                out=h1_grouped[n][:, h, tokens, :],
+                in0=v1[n][:, h, :, tokens].rearrange("p t m -> p m t"),
+                in1=e1[n][:].rearrange("p (h t m) -> p h t m", h=HALVES, t=PACK)[:, h, :, tokens].rearrange(
+                    "p t m -> p m t"
+                ),
                 op=ALU.mult,
-            )
-
-        def transpose_h1(n):
-            if not tile_ok(n):
-                return
-            words = h1[n][:].bitcast(F32)
-            h1_t[n] = psum_ht.tile([P, PASSES, 2, P], F32, name="h1_t")
-            for g in range(PASSES):
-                for u in range(2):
-                    nc.tensor.transpose(
-                        h1_t[n][:, g, u, :], words[:, g * WORDS + u : (g + 1) * WORDS : 2], ident_f32[:]
-                    )
-
-        def regroup_h1(n):
-            if not tile_ok(n):
-                return
-            h1_grouped[n] = triple.tile([P, PASSES, P, PACK], BF16, name="h1_grouped", align_bytes=64)
-            nc.scalar.copy(
-                out=h1_grouped[n][:].bitcast(F32), in_=h1_t[n][:].rearrange("p g u k -> p g k u")
             )
 
         def quantise_h1(n):
@@ -448,33 +456,34 @@ def tile_autoencoder_pa_t_kernel(
             mean_var = small.tile([P, 2, 2], F32, name="mean_var")
             passes_up_to(1)
             regroup_x(n + 5)
-            passes_up_to(2)
-            regroup_h1(m1)
-            if 0 <= n + 5 <= 2:
-                spread_rows(n + 5)
+            for h in range(HALVES):
+                if z_on_scalar(n + 1, h):
+                    normalise1(n + 1, h)
+            if n + 5 == 1:
+                spread_gains()
             while m0 is not None and m0 not in softplus_in_slot:
                 if next_pass(q) == 0:
                     raise AssertionError("product before its input")
             passes_up_to(RATE)
-            if G_COLS:
-                product1(m0, nc.gpsimd if n < N_TILES else nc.vector, slice(0, G_COLS))
-            centre1(n + 1, 0)
-            centre1(n + 1, 1)
+            for h in range(PASSES):
+                product1(m0, nc.gpsimd if n < N_TILES else nc.vector, h, slice(V_TOKENS, P))
+            affine1(n)
+            for h in range(HALVES):
+                if not z_on_scalar(n + 1, h):
+                    normalise1(n + 1, h)
             statistics1(n + 2)
-            statistics2(m3)
-            product1(m0, nc.vector, slice(G_COLS, D_HID))
-            transpose_h1(m0)
-            mean2_of(m3, mean_var)
+            statistics2(m2)
+            transpose_z(n + 1)
+            mean2_of(m2, mean_var)
             quantise_x(n + 3)
             layer1(n + 3)
             transpose_x(n + 6)
-            centre2(m3)
-            scale1(n)
-            quantise_h1(m2)
-            layer2(m2)
-            scale2(m4)
+            centre2(m2)
+            quantise_h1(m1)
+            layer2(m1)
+            scale2(m3)
             mean1_of(n + 2, mean_var)
-            inverse_std(n + 2, m3, mean_var)
+            inverse_std(n + 2, m2, mean_var)
             for e in finished2:
                 product2_and_store(e)
                 stored2.append(e)

@@ -22,6 +22,7 @@ HALVES = D_HID // K_PASS
 N_TILES = TOKENS // P
 BATCHES = [4, 4, 4, 4, 4, 4, 4, 4]
 TAIL_PAIRS = (14, 16)
+LINE = 4
 Z_EVERY = 2
 Z_WHICH = 1
 V_TOKENS = 0
@@ -326,11 +327,11 @@ def tile_autoencoder_pa_t_kernel(
             if n not in h1_grouped:
                 h1_grouped[n] = triple.tile([P, PASSES, P, PACK], BF16, name="h1_grouped", align_bytes=64)
             engine.tensor_tensor(
-                out=h1_grouped[n][:, h, tokens, :],
-                in0=v1[n][:, h, :, tokens].rearrange("p t m -> p m t"),
-                in1=e1[n][:].rearrange("p (h t m) -> p h t m", h=HALVES, t=PACK)[:, h, :, tokens].rearrange(
-                    "p t m -> p m t"
-                ),
+                out=h1_grouped[n][:, h, tokens, :].rearrange("p (c i) t -> p c t i", i=LINE),
+                in0=v1[n][:, h, :, tokens].rearrange("p t (c i) -> p c t i", i=LINE),
+                in1=e1[n][:]
+                .rearrange("p (h t m) -> p h t m", h=HALVES, t=PACK)[:, h, :, tokens]
+                .rearrange("p t (c i) -> p c t i", i=LINE),
                 op=ALU.mult,
             )
 

@@ -23,8 +23,10 @@ N_TILES = TOKENS // P
 BATCHES = [4, 4, 4, 4, 4, 4, 4, 4]
 TAIL_PAIRS = (14, 16)
 LINE = 4
-Z_EVERY = 2
-Z_WHICH = 1
+Z_HEAD = 5
+Z_TAIL = 24
+Z_EVERY = 4
+Z_WHICH = 3
 V_TOKENS = 0
 BEHIND = 7
 LAG = 2
@@ -257,7 +259,7 @@ def tile_autoencoder_pa_t_kernel(
                 rstd2[k] = rstd[:, 1:2]
 
         def z_on_scalar(n, h):
-            return h == 1 and n % Z_EVERY < Z_WHICH
+            return n < Z_HEAD or (h == 1 and n < Z_TAIL and n % Z_EVERY < Z_WHICH)
 
         def normalise1(n, h):
             if not tile_ok(n):
@@ -466,6 +468,8 @@ def tile_autoencoder_pa_t_kernel(
                 if next_pass(q) == 0:
                     raise AssertionError("product before its input")
             passes_up_to(RATE)
+            if n >= 0:
+                transpose_x(n + 6)
             for h in range(PASSES):
                 product1(m0, nc.gpsimd if n < N_TILES else nc.vector, h, slice(V_TOKENS, P))
             affine1(n)
@@ -478,7 +482,8 @@ def tile_autoencoder_pa_t_kernel(
             mean2_of(m2, mean_var)
             quantise_x(n + 3)
             layer1(n + 3)
-            transpose_x(n + 6)
+            if n < 0:
+                transpose_x(n + 6)
             centre2(m2)
             quantise_h1(m1)
             layer2(m1)

@@ -26,7 +26,7 @@ LINE = 4
 Z_HEAD = 5
 Z_TAIL = 24
 Z_EVERY = 4
-Z_WHICH = 3
+Z_WHICH = 0
 V_TOKENS = 0
 BEHIND = 7
 LAG = 2
@@ -211,12 +211,12 @@ def tile_autoencoder_pa_t_kernel(
                         stop=(g == PASSES - 1),
                     )
 
-        def statistics1(n):
+        def statistics1(n, h):
             if not tile_ok(n):
                 return
-            stats1[n] = small.tile([P, HALVES, STATS], F32, name="stats1")
-            for h in range(HALVES):
-                nc.vector.bn_stats(out=stats1[n][:, h, :], in_=u1[n, h][:])
+            if h == 0:
+                stats1[n] = small.tile([P, HALVES, STATS], F32, name="stats1")
+            nc.vector.bn_stats(out=stats1[n][:, h, :], in_=u1[n, h][:])
 
         def mean1_of(n, mean_var):
             if not tile_ok(n):
@@ -476,15 +476,16 @@ def tile_autoencoder_pa_t_kernel(
             for h in range(HALVES):
                 if not z_on_scalar(n + 1, h):
                     normalise1(n + 1, h)
-            statistics1(n + 2)
-            statistics2(m2)
             transpose_z(n + 1)
+            statistics2(m2)
+            statistics1(n + 2, 0)
             mean2_of(m2, mean_var)
+            statistics1(n + 2, 1)
+            centre2(m2)
             quantise_x(n + 3)
             layer1(n + 3)
             if n < 0:
                 transpose_x(n + 6)
-            centre2(m2)
             quantise_h1(m1)
             layer2(m1)
             scale2(m3)

@@ -23,6 +23,8 @@ N_TILES = TOKENS // P
 BATCHES = [4, 4, 4, 4, 4, 4, 4, 4]
 TAIL_PAIRS = (14, 16)
 LINE = 4
+X_FIRST = 8
+X_EVERY = 4
 Z_HEAD = 5
 Z_TAIL = 24
 Z_EVERY = 4
@@ -176,8 +178,10 @@ def tile_autoencoder_pa_t_kernel(
         def regroup_x(n):
             if not tile_ok(n):
                 return
+            on_vector = n >= X_FIRST and n % X_EVERY == X_EVERY - 1
+            copy = nc.vector.tensor_copy if on_vector else nc.scalar.copy
             x_grouped[n] = xgpool.tile([P, PASSES, P, PACK], BF16, name="x_grouped", align_bytes=64)
-            nc.scalar.copy(
+            copy(
                 out=x_grouped[n][:].bitcast(F32), in_=x_t[n][:].rearrange("p g u k -> p g k u")
             )
 
@@ -195,21 +199,20 @@ def tile_autoencoder_pa_t_kernel(
             x_scales[n] = triple.tile([P, PASSES, P], U8, name="x_scales", align_bytes=64)
             quantise(x_grouped[n][:], x_codes[n][:], x_scales[n][:])
 
-        def layer1(n):
+        def layer1(n, h):
             if not tile_ok(n):
                 return
-            for h in range(HALVES):
-                u1[n, h] = psum_u1.tile([P, K_PASS], F32, name="u1")
-                for g in range(PASSES):
-                    nc.tensor.matmul_mx(
-                        out=u1[n, h][:],
-                        lhsT=x_codes[n][:, g, :].bitcast(FP8X4),
-                        lhsT_scale=x_scales[n][:, g, :],
-                        rhs=w1_codes[:, g, PACK * K_PASS * h : PACK * K_PASS * (h + 1)].bitcast(FP8X4),
-                        rhs_scale=w1_scales[:, g, K_PASS * h : K_PASS * (h + 1)],
-                        start=(g == 0),
-                        stop=(g == PASSES - 1),
-                    )
+            u1[n, h] = psum_u1.tile([P, K_PASS], F32, name="u1")
+            for g in range(PASSES):
+                nc.tensor.matmul_mx(
+                    out=u1[n, h][:],
+                    lhsT=x_codes[n][:, g, :].bitcast(FP8X4),
+                    lhsT_scale=x_scales[n][:, g, :],
+                    rhs=w1_codes[:, g, PACK * K_PASS * h : PACK * K_PASS * (h + 1)].bitcast(FP8X4),
+                    rhs_scale=w1_scales[:, g, K_PASS * h : K_PASS * (h + 1)],
+                    start=(g == 0),
+                    stop=(g == PASSES - 1),
+                )
 
         def statistics1(n, h):
             if not tile_ok(n):
@@ -437,6 +440,11 @@ def tile_autoencoder_pa_t_kernel(
             return 1 if kind in ("half", "log", "softplus") else 0.01
 
         transpose_x(0)
+        regroup_x(0)
+        quantise_x(0)
+        layer1(0, 0)
+        transpose_x(1)
+        layer1(0, 1)
         q = -3
         while len(stored2) < N_TILES // GROUP2:
             q += 1
@@ -458,10 +466,11 @@ def tile_autoencoder_pa_t_kernel(
             place["done"] = 0
             mean_var = small.tile([P, 2, 2], F32, name="mean_var")
             passes_up_to(1)
-            regroup_x(n + 5)
             for h in range(HALVES):
                 if z_on_scalar(n + 1, h):
                     normalise1(n + 1, h)
+            if n + 5 > 0:
+                regroup_x(n + 5)
             if n + 5 == 1:
                 spread_gains()
             while m0 is not None and m0 not in softplus_in_slot:
@@ -482,9 +491,11 @@ def tile_autoencoder_pa_t_kernel(
             mean2_of(m2, mean_var)
             statistics1(n + 2, 1)
             centre2(m2)
-            quantise_x(n + 3)
-            layer1(n + 3)
-            if n < 0:
+            if n + 3 > 0:
+                quantise_x(n + 3)
+                for h in range(HALVES):
+                    layer1(n + 3, h)
+            if -5 < n < 0:
                 transpose_x(n + 6)
             quantise_h1(m1)
             layer2(m1)

from contextlib import ExitStack

import concourse.mybir as mybir
from concourse.masks import make_identity

F32 = mybir.dt.float32
BF16 = mybir.dt.bfloat16
I32 = mybir.dt.int32
U32 = mybir.dt.uint32
U8 = mybir.dt.uint8
FP8X4 = mybir.dt.float8_e4m3fn_x4
ACT = mybir.ActivationFunctionType
ALU = mybir.AluOpType

P = 128
PACK = 4
K_PASS = P * PACK
TOKENS, D_IN, D_HID, D_OUT = 4096, 1024, 1024, 256
WORDS = K_PASS // 2
PASSES = D_IN // K_PASS
HALVES = D_HID // K_PASS
N_TILES = TOKENS // P
BATCHES = [4, 4, 4, 4, 4, 4, 4, 4]
TAIL_PAIRS = (14, 16)
LINE = 4
X_FIRST = 8
X_EVERY = 4
Z_HEAD = 5
Z_TAIL = 24
Z_EVERY = 4
Z_WHICH = 0
V_TOKENS = 0
BEHIND = 7
LAG = 2
RATE = 3
GROUP2 = 2
X_AHEAD = 4
X_BUFS = 8
V_BUFS = 15
E_BUFS = 12
EPS = 1e-5
STATS = 6

FLOPS = 2 * TOKENS * D_IN * D_HID + 2 * TOKENS * D_HID * D_OUT


def tile_autoencoder_pa_t_kernel(
    tc, x, W1_words, W1_scales, g1, b1, W2_words, W2_scales, g2, b2, out
):
    nc = tc.nc
    with ExitStack() as stack:
        const = stack.enter_context(tc.tile_pool(name="const", bufs=1))
        pair = stack.enter_context(tc.tile_pool(name="pair", bufs=2))
        triple = stack.enter_context(tc.tile_pool(name="triple", bufs=3))
        v2pool = stack.enter_context(tc.tile_pool(name="v2pool", bufs=8))
        e2pool = stack.enter_context(tc.tile_pool(name="e2pool", bufs=8))
        xgpool = stack.enter_context(tc.tile_pool(name="xgpool", bufs=5))
        xpool = stack.enter_context(tc.tile_pool(name="xpool", bufs=X_BUFS))
        vpool = stack.enter_context(tc.tile_pool(name="vpool", bufs=V_BUFS))
        epool = stack.enter_context(tc.tile_pool(name="epool", bufs=E_BUFS))
        small = stack.enter_context(tc.tile_pool(name="small", bufs=6))
        psum_u1 = stack.enter_context(tc.psum_pool(name="psum_u1", bufs=2 * HALVES))
        psum_z = stack.enter_context(tc.psum_pool(name="psum_z", bufs=HALVES))
        psum_xt = stack.enter_context(tc.psum_pool(name="psum_xt", bufs=1))
        psum_u2 = stack.enter_context(tc.psum_pool(name="psum_u2", bufs=1))
        stack.enter_context(tc.manual_schedule())

        w1_scales = const.tile([P, PASSES, D_HID], U8, align_bytes=64)
        w2_scales = const.tile([P, PASSES, D_OUT], U8, align_bytes=64)
        nc.gpsimd.memset(w1_scales[:].bitcast(I32), 0)
        raw1 = []
        for row in (g1, b1):
            raw = const.tile([P, HALVES, PACK], BF16, name="raw_gain1" if row is g1 else "raw_bias1")
            nc.scalar.dma_start(out=raw[:], in_=row.rearrange("(h p t) -> p h t", h=HALVES, t=PACK))
            raw1.append(raw)
        rows2 = const.tile([P, 2, D_OUT], BF16)
        nc.vector.memset(rows2[:], 0.0)
        for j, row in enumerate((g2, b2)):
            nc.scalar.dma_start(out=rows2[0:1, j, :], in_=row.unsqueeze(0))
        nc.vector.memset(w2_scales[:].bitcast(I32), 0)
        ones = const.tile([P, P], BF16)
        nc.vector.memset(ones[:], 1.0)
        w1_codes = const.tile([P, PASSES, PACK * D_HID], U8, align_bytes=64)
        w2_codes = const.tile([P, PASSES, PACK * D_OUT], U8, align_bytes=64)

        def load_scales(plane, scales):
            for quadrant in range(4):
                nc.sync.dma_start(
                    out=plane[32 * quadrant : 32 * quadrant + 4, :, :].bitcast(I32),
                    in_=scales[:, 4 * quadrant : 4 * quadrant + 4, :]
                    .rearrange("g q n -> q g n")
                    .bitcast(I32),
                )

        def load_codes(codes, words):
            for g in range(PASSES):
                nc.sync.dma_start(
                    out=codes[:, g, :].bitcast(I32),
                    in_=words[g].rearrange("p n t -> p (n t)").bitcast(I32),
                )

        x_rows = {}

        def load_x(n):
            if not 0 <= n < N_TILES:
                return
            x_rows[n] = xpool.tile([P, D_IN], BF16, name="x_rows")
            nc.sync.dma_start(out=x_rows[n][:], in_=x[n * P : (n + 1) * P, :])

        load_x(0)
        load_scales(w1_scales, W1_scales)
        for h in range(HALVES):
            columns = slice(h * K_PASS, (h + 1) * K_PASS)
            for g in range(PASSES):
                nc.sync.dma_start(
                    out=w1_codes[:, g, PACK * h * K_PASS : PACK * (h + 1) * K_PASS].bitcast(I32),
                    in_=W1_words[g, :, columns, :].rearrange("p n t -> p (n t)").bitcast(I32),
                )
            load_x(h + 1)
        load_x(3)
        load_scales(w2_scales, W2_scales)
        load_codes(w2_codes, W2_words)

        ident_f32 = const.tile([P, P], F32)
        make_identity(nc, ident_f32[:])
        half = const.tile([P, 1], F32)
        nc.vector.memset(half[:], 0.5)
        minus_half = const.tile([P, 2], F32)
        nc.vector.memset(minus_half[:], -0.5)

        columns1 = const.tile([P, 2, HALVES, PACK], F32)
        gains2 = const.tile([P, 2, D_OUT], F32)

        def spread_gains():
            for j in range(2):
                nc.vector.tensor_copy(out=columns1[:, j], in_=raw1[j][:])
            spread = psum_z.tile([P, K_PASS], F32, name="z_t")
            nc.tensor.matmul(spread[:], lhsT=ones[:], rhs=rows2[:].rearrange("p j d -> p (j d)"), start=True, stop=True)
            nc.scalar.copy(out=gains2[:].rearrange("p j d -> p (j d)"), in_=spread[:])

        passes = []
        first = 0
        last_batch = []
        for size in BATCHES:
            batch = list(range(first, first + size))
            passes += [("softplus", n) for n in last_batch]
            passes.append(("tanh2", 0))
            passes += [("half", n) for n in batch]
            passes += [("log", n) for n in batch]
            passes.append(("log2", 0))
            last_batch = batch
            first += size
        passes += [("softplus", n) for n in last_batch]
        passes += [("tanh2", 0), ("log2", 0)]
        for pairs in TAIL_PAIRS:
            passes += [("wait2", pairs), ("tanh2", 0), ("log2", 0)]
        passes.append(("tanh2", 0))

        x_t, x_grouped, x_codes, x_scales = {}, {}, {}, {}
        u1, rstd1, mean1, shift1, stats1, z1, z_t, v1, e1 = {}, {}, {}, {}, {}, {}, {}, {}, {}
        h1_grouped, h1_codes, h1_scales = {}, {}, {}
        u2, rstd2, mean2, stats2, v2, e2 = {}, {}, {}, {}, {}, {}

        def tile_ok(n):
            return n is not None and 0 <= n < N_TILES

        def transpose_x(n):
            if not tile_ok(n):
                return
            words = x_rows[n][:].bitcast(F32)
            x_t[n] = psum_xt.tile([P, PASSES, 2, P], F32, name="x_t")
            for g in range(PASSES):
                for u in range(2):
                    nc.tensor.transpose(
                        x_t[n][:, g, u, :], words[:, g * WORDS + u : (g + 1) * WORDS : 2], ident_f32[:]
                    )

        def regroup_x(n):
            if not tile_ok(n):
                return
            on_vector = n >= X_FIRST and n % X_EVERY == X_EVERY - 1
            copy = nc.vector.tensor_copy if on_vector else nc.scalar.copy
            x_grouped[n] = xgpool.tile([P, PASSES, P, PACK], BF16, name="x_grouped", align_bytes=64)
            copy(
                out=x_grouped[n][:].bitcast(F32), in_=x_t[n][:].rearrange("p g u k -> p g k u")
            )

        def quantise(grouped, codes, scales):
            nc.vector.quantize_mx(
                out=codes.rearrange("p g k -> p (g k)").bitcast(FP8X4),
                scales=scales.rearrange("p g k -> p (g k)"),
                in_=grouped.rearrange("p g k t -> p (g k t)"),
            )

        def quantise_x(n):
            if not tile_ok(n):
                return
            x_codes[n] = triple.tile([P, PASSES, P], U32, name="x_codes", align_bytes=64)
            x_scales[n] = triple.tile([P, PASSES, P], U8, name="x_scales", align_bytes=64)
            quantise(x_grouped[n][:], x_codes[n][:], x_scales[n][:])

        def layer1(n, h):
            if not tile_ok(n):
                return
            u1[n, h] = psum_u1.tile([P, K_PASS], F32, name="u1")
            for g in range(PASSES):
                nc.tensor.matmul_mx(
                    out=u1[n, h][:],
                    lhsT=x_codes[n][:, g, :].bitcast(FP8X4),
                    lhsT_scale=x_scales[n][:, g, :],
                    rhs=w1_codes[:, g, PACK * K_PASS * h : PACK * K_PASS * (h + 1)].bitcast(FP8X4),
                    rhs_scale=w1_scales[:, g, K_PASS * h : K_PASS * (h + 1)],
                    start=(g == 0),
                    stop=(g == PASSES - 1),
                )

        def statistics1(n, h):
            if not tile_ok(n):
                return
            if h == 0:
                stats1[n] = small.tile([P, HALVES, STATS], F32, name="stats1")
            nc.vector.bn_stats(out=stats1[n][:, h, :], in_=u1[n, h][:])

        def mean1_of(n, mean_var):
            if not tile_ok(n):
                return
            nc.vector.bn_aggr(out=mean_var[:, 0, :], in_=stats1[n][:].rearrange("p j s -> p (j s)"))
            mean1[n] = mean_var[:, 0, 0:1]

        def mean2_of(n, mean_var):
            if not tile_ok(n):
                return
            nc.vector.bn_aggr(out=mean_var[:, 1, :], in_=stats2[n][:])
            mean2[n] = mean_var[:, 1, 0:1]

        def inverse_std(n, k, mean_var):
            first, last = (0 if tile_ok(n) else 1), (2 if tile_ok(k) else 1)
            if first == last:
                return
            shifted = small.tile([P, 2], F32, name="shifted")
            rstd = small.tile([P, 2], F32, name="rstd")
            nc.gpsimd.tensor_scalar(
                out=shifted[:, first:last],
                in0=mean_var[:, first:last, 1],
                scalar1=EPS,
                scalar2=1.0,
                op0=ALU.add,
                op1=ALU.mult,
            )
            nc.gpsimd.tensor_tensor(
                out=rstd[:, first:last], in0=shifted[:, first:last], in1=minus_half[:, first:last], op=ALU.pow
            )
            if tile_ok(n):
                rstd1[n] = rstd[:, 0:1]
                if z_on_scalar(n, 1):
                    shift = small.tile([P, 1], F32, name="shift")
                    nc.gpsimd.tensor_scalar(
                        out=shift[:], in0=mean_var[:, 0, 0:1], scalar1=rstd1[n], scalar2=-1.0, op0=ALU.mult, op1=ALU.mult
                    )
                    shift1[n] = shift[:, 0:1]
            if tile_ok(k):
                rstd2[k] = rstd[:, 1:2]

        def z_on_scalar(n, h):
            return n < Z_HEAD or (h == 1 and n < Z_TAIL and n % Z_EVERY < Z_WHICH)

        def normalise1(n, h):
            if not tile_ok(n):
                return
            if n not in z1:
                z1[n] = pair.tile([P, HALVES, PACK, P], F32, name="z1")
            if z_on_scalar(n, h):
                nc.scalar.activation(
                    out=z1[n][:, h],
                    in_=u1[n, h][:].rearrange("p (m t) -> p t m", t=PACK),
                    func=ACT.Identity,
                    scale=rstd1[n],
                    bias=shift1[n],
                )
            else:
                nc.vector.tensor_scalar(
                    out=z1[n][:, h],
                    in0=u1[n, h][:].rearrange("p (m t) -> p t m", t=PACK),
                    scalar1=mean1[n],
                    scalar2=rstd1[n],
                    op0=ALU.subtract,
                    op1=ALU.mult,
                )

        def transpose_z(n):
            if not tile_ok(n):
                return
            for h in range(HALVES):
                z_t[n, h] = psum_z.tile([P, PACK, P], F32, name="z_t")
                for t in range(PACK):
                    nc.tensor.transpose(z_t[n, h][:, t, :], z1[n][:, h, t, :], ident_f32[:])

        def affine1(n):
            if not tile_ok(n):
                return
            v1[n] = vpool.tile([P, HALVES, PACK, P], F32, name="v1")
            for h in range(HALVES):
                for t in range(PACK):
                    nc.vector.tensor_scalar(
                        out=v1[n][:, h, t, :],
                        in0=z_t[n, h][:, t, :],
                        scalar1=columns1[:, 0, h, t : t + 1],
                        scalar2=columns1[:, 1, h, t : t + 1],
                        op0=ALU.mult,
                        op1=ALU.add,
                    )
            scaled1.append(n)

        def tanh_half(e, v):
            nc.scalar.activation(out=e, in_=v, func=ACT.Tanh, scale=0.5)

        def log_of_rest(e):
            nc.scalar.activation(out=e, in_=e, func=ACT.Ln, scale=-0.5, bias=half[:, 0:1])

        def tanh_softplus(e):
            nc.scalar.activation(out=e, in_=e, func=ACT.Tanh, scale=-1.0)

        def tanh_half1(n):
            if not tile_ok(n):
                return
            e1[n] = epool.tile([P, D_HID], F32, name="e1")
            tanh_half(e1[n][:], v1[n][:].rearrange("p h t m -> p (h t m)"))

        def product1(n, engine, h, tokens):
            if not tile_ok(n):
                return
            if n not in h1_grouped:
                h1_grouped[n] = triple.tile([P, PASSES, P, PACK], BF16, name="h1_grouped", align_bytes=64)
            engine.tensor_tensor(
                out=h1_grouped[n][:, h, tokens, :].rearrange("p (c i) t -> p c t i", i=LINE),
                in0=v1[n][:, h, :, tokens].rearrange("p t (c i) -> p c t i", i=LINE),
                in1=e1[n][:]
                .rearrange("p (h t m) -> p h t m", h=HALVES, t=PACK)[:, h, :, tokens]
                .rearrange("p t (c i) -> p c t i", i=LINE),
                op=ALU.mult,
            )

        def quantise_h1(n):
            if not tile_ok(n):
                return
            h1_codes[n] = triple.tile([P, PASSES, P], U32, name="h1_codes", align_bytes=64)
            h1_scales[n] = triple.tile([P, PASSES, P], U8, name="h1_scales", align_bytes=64)
            quantise(h1_grouped[n][:], h1_codes[n][:], h1_scales[n][:])

        def layer2(n):
            if not tile_ok(n):
                return
            u2[n] = psum_u2.tile([P, D_OUT], F32, name="u2")
            for g in range(PASSES):
                nc.tensor.matmul_mx(
                    out=u2[n][:],
                    lhsT=h1_codes[n][:, g, :].bitcast(FP8X4),
                    lhsT_scale=h1_scales[n][:, g, :],
                    rhs=w2_codes[:, g, :].bitcast(FP8X4),
                    rhs_scale=w2_scales[:, g, :],
                    start=(g == 0),
                    stop=(g == PASSES - 1),
                )

        def statistics2(n):
            if not tile_ok(n):
                return
            stats2[n] = small.tile([P, STATS], F32, name="stats2")
            nc.vector.bn_stats(out=stats2[n][:], in_=u2[n][:])

        def centre2(n):
            if not tile_ok(n):
                return
            if n % GROUP2 == 0:
                v2[n // GROUP2] = v2pool.tile([P, GROUP2, D_OUT], F32, name="v2")
            nc.vector.scalar_tensor_tensor(
                out=v2[n // GROUP2][:, n % GROUP2, :],
                in0=u2[n][:],
                scalar=mean2[n],
                in1=gains2[:, 0, :],
                op0=ALU.subtract,
                op1=ALU.mult,
            )

        def scale2(n):
            if not tile_ok(n):
                return
            rows = v2[n // GROUP2][:, n % GROUP2, :]
            nc.vector.scalar_tensor_tensor(
                out=rows, in0=rows, scalar=rstd2[n], in1=gains2[:, 1, :], op0=ALU.mult, op1=ALU.add
            )
            if n % GROUP2 == GROUP2 - 1:
                scaled2.append(n // GROUP2)

        def flat2(tile2):
            return tile2[:].rearrange("p i d -> p (i d)")

        def product2_and_store(e):
            result = pair.tile([P, GROUP2, D_OUT], F32, name="result")
            nc.vector.tensor_tensor(out=flat2(result), in0=flat2(v2[e]), in1=flat2(e2[e]), op=ALU.mult)
            rows = out[e * GROUP2 * P : (e + 1) * GROUP2 * P, :]
            nc.sync.dma_start(out=rows.rearrange("(i p) d -> p i d", p=P), in_=result[:])

        scaled1, scaled2 = [], []
        waiting2, logged2, finished2 = [], [], []
        softplus_in_slot, product_slot, stored2 = {}, {}, []
        place = {"next": 0}

        def next_pass(q):
            if place["next"] == len(passes):
                return 0
            kind, n = passes[place["next"]]
            if kind == "half":
                if n not in scaled1:
                    return 0
                tanh_half1(n)
            if kind == "log":
                log_of_rest(e1[n][:])
            if kind == "softplus":
                tanh_softplus(e1[n][:])
                softplus_in_slot[n] = q
            if kind == "wait2" and len(stored2) + len(scaled2) + len(logged2) + len(waiting2) + len(finished2) < n:
                return 0
            if kind == "tanh2":
                for e in logged2:
                    tanh_softplus(flat2(e2[e]))
                    finished2.append(e)
                logged2.clear()
                for e in scaled2:
                    e2[e] = e2pool.tile([P, GROUP2, D_OUT], F32, name="e2")
                    tanh_half(flat2(e2[e]), flat2(v2[e]))
                    waiting2.append(e)
                scaled2.clear()
            if kind == "log2":
                for e in waiting2:
                    log_of_rest(flat2(e2[e]))
                    logged2.append(e)
                waiting2.clear()
            place["next"] += 1
            return 1 if kind in ("half", "log", "softplus") else 0.01

        transpose_x(0)
        regroup_x(0)
        quantise_x(0)
        layer1(0, 0)
        transpose_x(1)
        layer1(0, 1)
        q = -3
        while len(stored2) < N_TILES // GROUP2:
            q += 1
            n = q - 3
            made = len(product_slot)
            if made < N_TILES and n >= made + BEHIND or n > N_TILES:
                if made < N_TILES:
                    product_slot[made] = q
            m0, m1, m2, m3, m4 = ([k for k in product_slot if product_slot[k] == q - j] for j in range(5))
            m0, m1, m2, m3, m4 = ((m[0] if m else None) for m in (m0, m1, m2, m3, m4))
            load_x(n + 5 + X_AHEAD)
            def passes_up_to(share):
                while place["done"] < share:
                    weight = next_pass(q)
                    if weight == 0:
                        break
                    place["done"] += weight

            place["done"] = 0
            mean_var = small.tile([P, 2, 2], F32, name="mean_var")
            passes_up_to(1)
            for h in range(HALVES):
                if z_on_scalar(n + 1, h):
                    normalise1(n + 1, h)
            if n + 5 > 0:
                regroup_x(n + 5)
            if n + 5 == 1:
                spread_gains()
            while m0 is not None and m0 not in softplus_in_slot:
                if next_pass(q) == 0:
                    raise AssertionError("product before its input")
            passes_up_to(RATE)
            if n >= 0:
                transpose_x(n + 6)
            for h in range(PASSES):
                product1(m0, nc.gpsimd if n < N_TILES else nc.vector, h, slice(V_TOKENS, P))
            affine1(n)
            for h in range(HALVES):
                if not z_on_scalar(n + 1, h):
                    normalise1(n + 1, h)
            transpose_z(n + 1)
            statistics2(m2)
            statistics1(n + 2, 0)
            mean2_of(m2, mean_var)
            statistics1(n + 2, 1)
            centre2(m2)
            if n + 3 > 0:
                quantise_x(n + 3)
                for h in range(HALVES):
                    layer1(n + 3, h)
            if -5 < n < 0:
                transpose_x(n + 6)
            quantise_h1(m1)
            layer2(m1)
            scale2(m3)
            mean1_of(n + 2, mean_var)
            inverse_std(n + 2, m2, mean_var)
            for e in finished2:
                product2_and_store(e)
                stored2.append(e)
            finished2.clear()
